import numpy as np
import ml_dtypes


def mxq(x, axis, fmt="e4m3"):
    dtype, down = {"e4m3": (ml_dtypes.float8_e4m3fn, 7), "e5m2": (ml_dtypes.float8_e5m2, 14)}[fmt]
    v = np.moveaxis(np.asarray(x, np.float32).astype(ml_dtypes.bfloat16).astype(np.float64), axis, -1)
    blocks = v.reshape(v.shape[:-1] + (-1, 32))
    amax = np.abs(blocks).max(-1, keepdims=True)
    byte = np.maximum(np.where(amax > 0, np.frexp(amax)[1] - 1 + 127, 0) - down, 1)
    scale = np.exp2(byte - 127.0)
    codes = (blocks / scale).astype(np.float32).astype(dtype).astype(np.float64)
    return np.moveaxis((codes * scale).reshape(v.shape), -1, axis)


WIDE = False


def mx_kscale(k):
    if not WIDE:
        return np.ones(k)
    levels = np.array([10, -10, 5, -5, 0])
    a = np.random.permutation(np.resize(levels, k // 512 * 4)).reshape(k // 512, 4)
    idx = np.arange(k)
    return np.exp2(a[idx // 512, idx % 128 // 32])


BF16 = ml_dtypes.bfloat16


def bf(x):
    return np.asarray(x, np.float32).astype(BF16)


def f64(x):
    return np.asarray(x).astype(np.float64)


E2M1 = np.array([0.0, 0.5, 1.0, 1.5, 2.0, 3.0, 4.0, 6.0, -0.0, -0.5, -1.0, -1.5, -2.0, -3.0, -4.0, -6.0])


def pack_weight(w, fmt):
    k, n = w.shape
    w = f64(bf(w)).reshape(k // 32, 32, n)
    amax = np.abs(w).max(1)
    if fmt == "e4m3":
        byte = np.frexp(amax)[1] - 1 + 127 - 7
    else:
        mant, ex = np.frexp(amax / 6.0)
        byte = np.where(mant > 0.5, ex, ex - 1) + 127
    byte = np.clip(np.where(amax > 0, byte, 1), 1, 254)
    scaled = (w * np.exp2(127.0 - byte)[:, None, :]).reshape(k, n).astype(np.float32)
    by_word = np.ascontiguousarray(scaled.reshape(k // 512, 128, 4, n).transpose(0, 1, 3, 2))
    if fmt == "e4m3":
        words = by_word.astype(ml_dtypes.float8_e4m3fn).view(np.uint8)
    else:
        c = by_word.astype(ml_dtypes.float4_e2m1fn).view(np.uint8) & 0xF
        words = c[..., 0::2] | (c[..., 1::2] << 4)
    return np.ascontiguousarray(words), np.ascontiguousarray(byte.astype(np.uint8).reshape(k // 512, 16, n))


def unpack_weight(words, scales, fmt):
    g, p, n, _ = words.shape
    if fmt == "e4m3":
        vals = np.ascontiguousarray(words).view(ml_dtypes.float8_e4m3fn).astype(np.float64)
    else:
        nib = np.empty((g, p, n, 4), np.uint8)
        nib[..., 0::2] = words & 0xF
        nib[..., 1::2] = words >> 4
        vals = E2M1[nib]
    vals = vals * np.repeat(np.exp2(scales.astype(np.float64) - 127.0), 8, axis=1)[..., None]
    return vals.transpose(0, 1, 3, 2).reshape(g * 512, n)

def pack4(w):
    words, scales = pack_weight(w, "e2m1")
    return words.reshape(words.shape[0], 128, -1), scales


def unpack4(words, scales):
    return unpack_weight(words.reshape(words.shape[0], 128, -1, 2), scales, "e2m1")


BS, D, R = 512, 2048, 2048
ALPHA = 1.0


def setup_inputs():
    s = mx_kscale(D)
    f = np.random.standard_normal((BS, D)) + np.random.standard_normal((BS, 1)) * np.random.standard_normal((1, D))
    features = bf(f * s)
    words, scales = pack4(np.random.standard_normal((D, R)) * np.sqrt(0.5 / (D * R)) / s[:, None])
    return {"features": features, "P_words": words, "P_scales": scales}


def reference(features, P_words, P_scales):
    Z = mxq(f64(features), 1, "e4m3") @ unpack4(P_words, P_scales)
    sq_norm = np.sum(Z * Z, axis=1)
    Zq = mxq(Z, 1, "e4m3")
    sq = sq_norm[:, None] + sq_norm[None, :] - 2.0 * (Zq @ Zq.T)
    sq = np.maximum(sq, 0.0)
    eye = np.eye(Z.shape[0], dtype=bool)
    dist = np.where(eye, 0.0, np.sqrt(np.where(eye, 1.0, sq)))
    adjacency_pre = np.exp(-ALPHA * dist)
    d_inv_sqrt = 1.0 / np.sqrt(np.sum(adjacency_pre, axis=1))
    normalized = d_inv_sqrt[:, None] * adjacency_pre * d_inv_sqrt[None, :]
    return (normalized, adjacency_pre)

@@ -1,0 +1,206 @@
+from contextlib import ExitStack
+
+import concourse.mybir as mybir
+from concourse.masks import make_identity
+
+F32 = mybir.dt.float32
+BF16 = mybir.dt.bfloat16
+I32 = mybir.dt.int32
+U32 = mybir.dt.uint32
+U8 = mybir.dt.uint8
+FP8X4 = mybir.dt.float8_e4m3fn_x4
+FP4X4 = mybir.dt.float4_e2m1fn_x4
+ACT = mybir.ActivationFunctionType
+ALU = mybir.AluOpType
+
+P = 128
+PACK = 4
+K_PASS = P * PACK
+BS, D, R = 512, 2048, 2048
+ROW_BLOCKS = BS // P
+D_PASSES = D // K_PASS
+R_PASSES = R // K_PASS
+SQRT_FLOOR = 2.0 ** -116
+
+FLOPS = 2 * BS * D * R + 2 * BS * BS * R
+
+
+def tile_metric_learning_based_adjacency_matrix_kernel(tc, features, P_words, P_scales, out_0, out_1):
+    nc = tc.nc
+    with ExitStack() as ctx:
+        keep = ctx.enter_context(tc.tile_pool(name="keep", bufs=1))
+        work = ctx.enter_context(tc.tile_pool(name="work", bufs=4))
+        banks = ctx.enter_context(tc.psum_pool(name="banks", bufs=4))
+        gram_pool = ctx.enter_context(tc.psum_pool(name="gram", bufs=1))
+
+        p_planes = keep.tile([P, D_PASSES, R], U8, align_bytes=64)
+        nc.vector.memset(p_planes[:].rearrange("p g n -> p (g n)").bitcast(I32), 0)
+        sqrt_floor = keep.tile([P, 1], F32)
+        nc.vector.memset(sqrt_floor[:], SQRT_FLOOR)
+        minus_half = keep.tile([P, 1], F32)
+        nc.vector.memset(minus_half[:], -0.5)
+        ones = keep.tile([P, P], F32)
+        nc.vector.memset(ones[:], 1.0)
+        ident = keep.tile([P, P], F32)
+        make_identity(nc, ident[:])
+        off_diag = keep.tile([P, P], F32)
+        nc.vector.tensor_scalar(out=off_diag[:], in0=ident[:], scalar1=-1.0, scalar2=1.0, op0=ALU.mult, op1=ALU.add)
+        warm = keep.tile([P, 1], F32)
+        nc.scalar.activation(out=warm[:], in_=ones[:, 0:1], func=ACT.Sqrt)
+
+        x_sb = []
+        for ib in range(ROW_BLOCKS):
+            x_blk = keep.tile([P, D], BF16, name="x%d" % ib)
+            nc.sync.dma_start(out=x_blk[:], in_=features[ib * P : (ib + 1) * P, :])
+            x_sb.append(x_blk)
+        scales_i32 = P_scales.bitcast(I32)
+        for g0 in range(0, D_PASSES, 2):
+            for q in range(8):
+                first = 32 * (q // 4) + q % 4
+                nc.sync.dma_start(
+                    out=p_planes[first : P : 64, g0 : g0 + 2, :].bitcast(I32),
+                    in_=scales_i32[g0 : g0 + 2, q : 16 : 8, :].rearrange("g q n -> q g n"),
+                )
+        words_i32 = P_words.bitcast(I32)
+        p_words = []
+        for c in range(R_PASSES):
+            chunk = keep.tile([P, D_PASSES, 2 * K_PASS], U8, name="pw%d" % c, align_bytes=64)
+            nc.sync.dma_start(
+                out=chunk[:].bitcast(I32),
+                in_=words_i32[:, :, c * (K_PASS // 2) : (c + 1) * (K_PASS // 2)].rearrange("g p w -> p g w"),
+            )
+            p_words.append(chunk)
+
+        f_grouped = [keep.tile([P, BS, PACK], BF16, name="fg%d" % g, align_bytes=64) for g in range(D_PASSES)]
+        f_codes = [keep.tile([P, BS], U32, name="fc%d" % g, align_bytes=64) for g in range(D_PASSES)]
+        f_scales = [keep.tile([P, BS], U8, name="fs%d" % g, align_bytes=64) for g in range(D_PASSES)]
+        HALF = BS // 2
+        for h in range(2):
+            flipped = [banks.tile([P, 2, 2, P], F32, name="flip%d" % g, tag="bank") for g in range(D_PASSES)]
+            for j in range(2):
+                x_words = x_sb[2 * h + j][:].bitcast(F32)
+                for g in range(D_PASSES):
+                    for u in range(2):
+                        nc.tensor.transpose(
+                            flipped[g][:, u, j, :], x_words[:, 256 * g + u : 256 * (g + 1) : 2], ident[:]
+                        )
+            cols = slice(h * HALF, (h + 1) * HALF)
+            for g in range(D_PASSES):
+                pairs = f_grouped[g][:].rearrange("p i t -> p (i t)").bitcast(F32).rearrange("p (i u) -> p i u", u=2)
+                source = flipped[g][:].rearrange("p u j i -> p (j i) u")
+                if g % 2 == 0:
+                    nc.vector.tensor_copy(out=pairs[:, cols, :], in_=source)
+                else:
+                    nc.scalar.copy(out=pairs[:, cols, :], in_=source)
+            for g in range(D_PASSES):
+                nc.vector.quantize_mx(
+                    out=f_codes[g][:, cols].bitcast(FP8X4),
+                    scales=f_scales[g][:, cols],
+                    in_=f_grouped[g][:, cols, :].rearrange("p i t -> p (i t)"),
+                )
+
+        z_grouped = [keep.tile([P, BS, PACK], BF16, name="zg%d" % c, align_bytes=64) for c in range(R_PASSES)]
+        z_codes = [keep.tile([P, BS], U32, name="zc%d" % c, align_bytes=64) for c in range(R_PASSES)]
+        z_scales = [keep.tile([P, BS], U8, name="zs%d" % c, align_bytes=64) for c in range(R_PASSES)]
+        squares = [keep.tile([P, PACK * P], F32, name="sq%d" % ib) for ib in range(ROW_BLOCKS)]
+        gram = [gram_pool.tile([P, BS], F32, name="gram%d" % ib) for ib in range(ROW_BLOCKS)]
+        for c in range(R_PASSES):
+            for ib in range(ROW_BLOCKS):
+                rows = slice(ib * P, (ib + 1) * P)
+                zt = banks.tile([P, PACK, P], F32, tag="bank")
+                for t in range(PACK):
+                    for g in range(D_PASSES):
+                        nc.tensor.matmul_mx(
+                            out=zt[:, t, :],
+                            lhsT=p_words[c][:, g, 2 * P * t : 2 * P * (t + 1)].bitcast(FP4X4),
+                            lhsT_scale=p_planes[:, g, c * K_PASS + t * P : c * K_PASS + (t + 1) * P],
+                            rhs=f_codes[g][:, rows].bitcast(FP8X4),
+                            rhs_scale=f_scales[g][:, rows],
+                            start=(g == 0),
+                            stop=(g == D_PASSES - 1),
+                        )
+                regrouped = zt[:].rearrange("p t i -> p i t")
+                if ib % 2 == 0:
+                    nc.vector.tensor_copy(out=z_grouped[c][:, rows, :], in_=regrouped)
+                else:
+                    nc.scalar.copy(out=z_grouped[c][:, rows, :], in_=regrouped)
+                flat = zt[:].rearrange("p t i -> p (t i)")
+                if c == 0:
+                    nc.scalar.activation(out=squares[ib][:], in_=flat, func=ACT.Square)
+                else:
+                    fresh = work.tile([P, PACK * P], F32, tag="fresh")
+                    nc.scalar.activation(out=fresh[:], in_=flat, func=ACT.Square)
+                    nc.vector.tensor_add(out=squares[ib][:], in0=squares[ib][:], in1=fresh[:])
+                nc.vector.quantize_mx(
+                    out=z_codes[c][:, rows].bitcast(FP8X4),
+                    scales=z_scales[c][:, rows],
+                    in_=z_grouped[c][:, rows, :].rearrange("p i t -> p (i t)"),
+                )
+            for ib in range(ROW_BLOCKS):
+                rows = slice(ib * P, (ib + 1) * P)
+                nc.tensor.matmul_mx(
+                    out=gram[ib][:],
+                    lhsT=z_codes[c][:, rows].bitcast(FP8X4),
+                    lhsT_scale=z_scales[c][:, rows],
+                    rhs=z_codes[c][:].bitcast(FP8X4),
+                    rhs_scale=z_scales[c][:],
+                    start=(c == 0),
+                    stop=(c == R_PASSES - 1),
+                )
+
+        col_sums = keep.tile([P, BS], F32)
+        n_rows_ps = banks.tile([P, BS], F32, tag="bank")
+        n_col_ps = banks.tile([P, ROW_BLOCKS], F32, tag="bank")
+        for ib in range(ROW_BLOCKS):
+            rows = slice(ib * P, (ib + 1) * P)
+            sq = squares[ib]
+            nc.vector.tensor_add(out=sq[:, 0 : 2 * P], in0=sq[:, 0 : 2 * P], in1=sq[:, 2 * P : 4 * P])
+            nc.vector.tensor_add(out=col_sums[:, rows], in0=sq[:, 0:P], in1=sq[:, P : 2 * P])
+            nc.tensor.matmul(out=n_rows_ps[:, rows], lhsT=ones[:], rhs=col_sums[:, rows], start=True, stop=True)
+            nc.tensor.matmul(out=n_col_ps[:, ib : ib + 1], lhsT=col_sums[:, rows], rhs=ones[:, 0:1], start=True, stop=True)
+        n_rows = keep.tile([P, BS], F32)
+        nc.scalar.copy(out=n_rows[:], in_=n_rows_ps[:])
+        n_col = keep.tile([P, ROW_BLOCKS], F32)
+        nc.vector.tensor_copy(out=n_col[:], in_=n_col_ps[:])
+
+        dist = [keep.tile([P, BS], F32, name="dist%d" % ib) for ib in range(ROW_BLOCKS)]
+        for ib in range(ROW_BLOCKS):
+            rows = slice(ib * P, (ib + 1) * P)
+            sq_dist = work.tile([P, BS], F32, tag="sq_dist")
+            nc.vector.scalar_tensor_tensor(
+                out=sq_dist[:], in0=gram[ib][:], scalar=-2.0, in1=n_rows[:], op0=ALU.mult, op1=ALU.add
+            )
+            nc.vector.tensor_scalar(
+                out=sq_dist[:], in0=sq_dist[:], scalar1=n_col[:, ib : ib + 1], scalar2=0.0, op0=ALU.add, op1=ALU.max
+            )
+            nc.vector.tensor_mul(out=sq_dist[:, rows], in0=sq_dist[:, rows], in1=off_diag[:])
+            nc.scalar.activation(out=dist[ib][:], in_=sq_dist[:], func=ACT.Sqrt, bias=sqrt_floor[:])
+
+        adj = [keep.tile([P, BS], F32, name="adj%d" % ib) for ib in range(ROW_BLOCKS)]
+        deg = keep.tile([P, ROW_BLOCKS], F32)
+        inv_sqrt_deg = keep.tile([P, ROW_BLOCKS], F32)
+        inv_rows_ps = banks.tile([P, BS], F32, tag="bank")
+        for ib in range(ROW_BLOCKS):
+            rows = slice(ib * P, (ib + 1) * P)
+            one = slice(ib, ib + 1)
+            nc.scalar.activation(out=adj[ib][:], in_=dist[ib][:], func=ACT.Exp, scale=-1.0, accum_out=deg[:, one])
+            nc.vector.scalar_tensor_tensor(
+                out=adj[ib][:, rows], in0=adj[ib][:, rows], scalar=1.0, in1=ident[:], op0=ALU.min, op1=ALU.max
+            )
+            nc.sync.dma_start(out=out_1[rows, :], in_=adj[ib][:])
+            nc.gpsimd.tensor_tensor(out=inv_sqrt_deg[:, one], in0=deg[:, one], in1=minus_half[:], op=ALU.pow)
+            nc.tensor.matmul(
+                out=inv_rows_ps[:, rows], lhsT=inv_sqrt_deg[:, one].to_broadcast([P, P]), rhs=ident[:], start=True, stop=True
+            )
+        for ib in range(ROW_BLOCKS):
+            rows = slice(ib * P, (ib + 1) * P)
+            normalized = work.tile([P, BS], F32, tag="normalized")
+            nc.vector.scalar_tensor_tensor(
+                out=normalized[:],
+                in0=adj[ib][:],
+                scalar=inv_sqrt_deg[:, ib : ib + 1],
+                in1=inv_rows_ps[:],
+                op0=ALU.mult,
+                op1=ALU.mult,
+            )
+            nc.sync.dma_start(out=out_0[rows, :], in_=normalized[:])

@@ -32,6 +32,7 @@ def tile_metric_learning_based_adjacency_matrix_kernel(tc, features, P_words, P_
         work = ctx.enter_context(tc.tile_pool(name="work", bufs=4))
         banks = ctx.enter_context(tc.psum_pool(name="banks", bufs=4))
         gram_pool = ctx.enter_context(tc.psum_pool(name="gram", bufs=1))
+        ctx.enter_context(tc.manual_schedule())
 
         p_planes = keep.tile([P, D_PASSES, R], U8, align_bytes=64)
         nc.vector.memset(p_planes[:].rearrange("p g n -> p (g n)").bitcast(I32), 0)
@@ -54,16 +55,14 @@ def tile_metric_learning_based_adjacency_matrix_kernel(tc, features, P_words, P_
             nc.sync.dma_start(out=x_blk[:], in_=features[ib * P : (ib + 1) * P, :])
             x_sb.append(x_blk)
         scales_i32 = P_scales.bitcast(I32)
-        for g0 in range(0, D_PASSES, 2):
-            for q in range(8):
-                first = 32 * (q // 4) + q % 4
-                nc.sync.dma_start(
-                    out=p_planes[first : P : 64, g0 : g0 + 2, :].bitcast(I32),
-                    in_=scales_i32[g0 : g0 + 2, q : 16 : 8, :].rearrange("g q n -> q g n"),
-                )
         words_i32 = P_words.bitcast(I32)
         p_words = []
         for c in range(R_PASSES):
+            for q in range(4):
+                nc.sync.dma_start(
+                    out=p_planes[q : P : 32, :, c * K_PASS : (c + 1) * K_PASS].bitcast(I32),
+                    in_=scales_i32[:, q : 16 : 4, c * (K_PASS // 4) : (c + 1) * (K_PASS // 4)].rearrange("g q n -> q g n"),
+                )
             chunk = keep.tile([P, D_PASSES, 2 * K_PASS], U8, name="pw%d" % c, align_bytes=64)
             nc.sync.dma_start(
                 out=chunk[:].bitcast(I32),
@@ -104,38 +103,59 @@ def tile_metric_learning_based_adjacency_matrix_kernel(tc, features, P_words, P_
         z_scales = [keep.tile([P, BS], U8, name="zs%d" % c, align_bytes=64) for c in range(R_PASSES)]
         squares = [keep.tile([P, PACK * P], F32, name="sq%d" % ib) for ib in range(ROW_BLOCKS)]
         gram = [gram_pool.tile([P, BS], F32, name="gram%d" % ib) for ib in range(ROW_BLOCKS)]
-        for c in range(R_PASSES):
-            for ib in range(ROW_BLOCKS):
-                rows = slice(ib * P, (ib + 1) * P)
-                zt = banks.tile([P, PACK, P], F32, tag="bank")
-                for t in range(PACK):
-                    for g in range(D_PASSES):
-                        nc.tensor.matmul_mx(
-                            out=zt[:, t, :],
-                            lhsT=p_words[c][:, g, 2 * P * t : 2 * P * (t + 1)].bitcast(FP4X4),
-                            lhsT_scale=p_planes[:, g, c * K_PASS + t * P : c * K_PASS + (t + 1) * P],
-                            rhs=f_codes[g][:, rows].bitcast(FP8X4),
-                            rhs_scale=f_scales[g][:, rows],
-                            start=(g == 0),
-                            stop=(g == D_PASSES - 1),
-                        )
-                regrouped = zt[:].rearrange("p t i -> p i t")
-                if ib % 2 == 0:
-                    nc.vector.tensor_copy(out=z_grouped[c][:, rows, :], in_=regrouped)
-                else:
-                    nc.scalar.copy(out=z_grouped[c][:, rows, :], in_=regrouped)
-                flat = zt[:].rearrange("p t i -> p (t i)")
-                if c == 0:
-                    nc.scalar.activation(out=squares[ib][:], in_=flat, func=ACT.Square)
-                else:
-                    fresh = work.tile([P, PACK * P], F32, tag="fresh")
-                    nc.scalar.activation(out=fresh[:], in_=flat, func=ACT.Square)
-                    nc.vector.tensor_add(out=squares[ib][:], in0=squares[ib][:], in1=fresh[:])
-                nc.vector.quantize_mx(
-                    out=z_codes[c][:, rows].bitcast(FP8X4),
-                    scales=z_scales[c][:, rows],
-                    in_=z_grouped[c][:, rows, :].rearrange("p i t -> p (i t)"),
-                )
+        col_sums = keep.tile([P, BS], F32)
+        n_rows = keep.tile([P, BS], F32)
+        n_col = keep.tile([P, ROW_BLOCKS], F32)
+        def project(c, ib):
+            rows = slice(ib * P, (ib + 1) * P)
+            zt = banks.tile([P, PACK, P], F32, tag="bank")
+            for t in range(PACK):
+                for g in range(D_PASSES):
+                    nc.tensor.matmul_mx(
+                        out=zt[:, t, :],
+                        lhsT=p_words[c][:, g, 2 * P * t : 2 * P * (t + 1)].bitcast(FP4X4),
+                        lhsT_scale=p_planes[:, g, c * K_PASS + t * P : c * K_PASS + (t + 1) * P],
+                        rhs=f_codes[g][:, rows].bitcast(FP8X4),
+                        rhs_scale=f_scales[g][:, rows],
+                        start=(g == 0),
+                        stop=(g == D_PASSES - 1),
+                    )
+            return zt
+
+        def empty_bank(c, ib, zt):
+            rows = slice(ib * P, (ib + 1) * P)
+            fresh = squares[ib] if c == 0 else work.tile([P, PACK * P], F32, name="fresh", tag="fresh")
+            nc.scalar.activation(out=fresh[:], in_=zt[:].rearrange("p t i -> p (t i)"), func=ACT.Square)
+            regrouped = zt[:].rearrange("p t i -> p i t")
+            if ib % 2 == 0:
+                nc.scalar.copy(out=z_grouped[c][:, rows, :], in_=regrouped)
+            else:
+                nc.vector.tensor_copy(out=z_grouped[c][:, rows, :], in_=regrouped)
+            return fresh
+
+        def quantise_and_add(c, ib, fresh):
+            rows = slice(ib * P, (ib + 1) * P)
+            nc.vector.quantize_mx(
+                out=z_codes[c][:, rows].bitcast(FP8X4),
+                scales=z_scales[c][:, rows],
+                in_=z_grouped[c][:, rows, :].rearrange("p i t -> p (i t)"),
+            )
+            if c > 0:
+                nc.vector.tensor_add(out=squares[ib][:], in0=squares[ib][:], in1=fresh[:])
+            if c == R_PASSES - 1:
+                sq = squares[ib]
+                nc.vector.tensor_add(out=sq[:, 0 : 2 * P], in0=sq[:, 0 : 2 * P], in1=sq[:, 2 * P : 4 * P])
+                nc.vector.tensor_add(out=col_sums[:, rows], in0=sq[:, 0:P], in1=sq[:, P : 2 * P])
+
+        def norms(ib):
+            rows = slice(ib * P, (ib + 1) * P)
+            one = slice(ib, ib + 1)
+            nc.tensor.matmul(out=n_rows_ps[:, rows], lhsT=ones[:], rhs=col_sums[:, rows], start=True, stop=True)
+            nc.tensor.matmul(out=n_col_ps[:, one], lhsT=col_sums[:, rows], rhs=ones[:, 0:1], start=True, stop=True)
+            nc.scalar.copy(out=n_rows[:, rows], in_=n_rows_ps[:, rows])
+            nc.vector.tensor_copy(out=n_col[:, one], in_=n_col_ps[:, one])
+
+        def gram_passes(c):
             for ib in range(ROW_BLOCKS):
                 rows = slice(ib * P, (ib + 1) * P)
                 nc.tensor.matmul_mx(
@@ -148,20 +168,22 @@ def tile_metric_learning_based_adjacency_matrix_kernel(tc, features, P_words, P_
                     stop=(c == R_PASSES - 1),
                 )
 
-        col_sums = keep.tile([P, BS], F32)
+        waiting = None
+        for c in range(R_PASSES):
+            for ib in range(ROW_BLOCKS):
+                zt = project(c, ib)
+                if waiting is not None:
+                    quantise_and_add(*waiting)
+                waiting = (c, ib, empty_bank(c, ib, zt))
+                if c > 0 and ib == 1:
+                    gram_passes(c - 1)
         n_rows_ps = banks.tile([P, BS], F32, tag="bank")
         n_col_ps = banks.tile([P, ROW_BLOCKS], F32, tag="bank")
-        for ib in range(ROW_BLOCKS):
-            rows = slice(ib * P, (ib + 1) * P)
-            sq = squares[ib]
-            nc.vector.tensor_add(out=sq[:, 0 : 2 * P], in0=sq[:, 0 : 2 * P], in1=sq[:, 2 * P : 4 * P])
-            nc.vector.tensor_add(out=col_sums[:, rows], in0=sq[:, 0:P], in1=sq[:, P : 2 * P])
-            nc.tensor.matmul(out=n_rows_ps[:, rows], lhsT=ones[:], rhs=col_sums[:, rows], start=True, stop=True)
-            nc.tensor.matmul(out=n_col_ps[:, ib : ib + 1], lhsT=col_sums[:, rows], rhs=ones[:, 0:1], start=True, stop=True)
-        n_rows = keep.tile([P, BS], F32)
-        nc.scalar.copy(out=n_rows[:], in_=n_rows_ps[:])
-        n_col = keep.tile([P, ROW_BLOCKS], F32)
-        nc.vector.tensor_copy(out=n_col[:], in_=n_col_ps[:])
+        quantise_and_add(*waiting)
+        for ib in range(ROW_BLOCKS - 1):
+            norms(ib)
+        gram_passes(R_PASSES - 1)
+        norms(ROW_BLOCKS - 1)
 
         dist = [keep.tile([P, BS], F32, name="dist%d" % ib) for ib in range(ROW_BLOCKS)]
         for ib in range(ROW_BLOCKS):
@@ -173,8 +195,10 @@ def tile_metric_learning_based_adjacency_matrix_kernel(tc, features, P_words, P_
             nc.vector.tensor_scalar(
                 out=sq_dist[:], in0=sq_dist[:], scalar1=n_col[:, ib : ib + 1], scalar2=0.0, op0=ALU.add, op1=ALU.max
             )
-            nc.vector.tensor_mul(out=sq_dist[:, rows], in0=sq_dist[:, rows], in1=off_diag[:])
             nc.scalar.activation(out=dist[ib][:], in_=sq_dist[:], func=ACT.Sqrt, bias=sqrt_floor[:])
+        for ib in range(ROW_BLOCKS):
+            rows = slice(ib * P, (ib + 1) * P)
+            nc.vector.tensor_mul(out=dist[ib][:, rows], in0=dist[ib][:, rows], in1=off_diag[:])
 
         adj = [keep.tile([P, BS], F32, name="adj%d" % ib) for ib in range(ROW_BLOCKS)]
         deg = keep.tile([P, ROW_BLOCKS], F32)

@@ -144,16 +144,14 @@ def tile_metric_learning_based_adjacency_matrix_kernel(tc, features, P_words, P_
                 nc.vector.tensor_add(out=squares[ib][:], in0=squares[ib][:], in1=fresh[:])
             if c == R_PASSES - 1:
                 sq = squares[ib]
-                nc.vector.tensor_add(out=sq[:, 0 : 2 * P], in0=sq[:, 0 : 2 * P], in1=sq[:, 2 * P : 4 * P])
-                nc.vector.tensor_add(out=col_sums[:, rows], in0=sq[:, 0:P], in1=sq[:, P : 2 * P])
+                nc.gpsimd.tensor_tensor(out=sq[:, 0 : 2 * P], in0=sq[:, 0 : 2 * P], in1=sq[:, 2 * P : 4 * P], op=ALU.add)
+                nc.gpsimd.tensor_tensor(out=col_sums[:, rows], in0=sq[:, 0:P], in1=sq[:, P : 2 * P], op=ALU.add)
 
         def norms(ib):
             rows = slice(ib * P, (ib + 1) * P)
             one = slice(ib, ib + 1)
             nc.tensor.matmul(out=n_rows_ps[:, rows], lhsT=ones[:], rhs=col_sums[:, rows], start=True, stop=True)
             nc.tensor.matmul(out=n_col_ps[:, one], lhsT=col_sums[:, rows], rhs=ones[:, 0:1], start=True, stop=True)
-            nc.scalar.copy(out=n_rows[:, rows], in_=n_rows_ps[:, rows])
-            nc.vector.tensor_copy(out=n_col[:, one], in_=n_col_ps[:, one])
 
         def gram_passes(c):
             for ib in range(ROW_BLOCKS):
@@ -175,8 +173,8 @@ def tile_metric_learning_based_adjacency_matrix_kernel(tc, features, P_words, P_
                 if waiting is not None:
                     quantise_and_add(*waiting)
                 waiting = (c, ib, empty_bank(c, ib, zt))
-                if c > 0 and ib == 1:
-                    gram_passes(c - 1)
+            if c > 0:
+                gram_passes(c - 1)
         n_rows_ps = banks.tile([P, BS], F32, tag="bank")
         n_col_ps = banks.tile([P, ROW_BLOCKS], F32, tag="bank")
         quantise_and_add(*waiting)
@@ -184,6 +182,8 @@ def tile_metric_learning_based_adjacency_matrix_kernel(tc, features, P_words, P_
             norms(ib)
         gram_passes(R_PASSES - 1)
         norms(ROW_BLOCKS - 1)
+        nc.scalar.copy(out=n_rows[:], in_=n_rows_ps[:])
+        nc.vector.tensor_copy(out=n_col[:], in_=n_col_ps[:])
 
         dist = [keep.tile([P, BS], F32, name="dist%d" % ib) for ib in range(ROW_BLOCKS)]
         for ib in range(ROW_BLOCKS):

@@ -98,60 +98,49 @@ def tile_metric_learning_based_adjacency_matrix_kernel(tc, features, P_words, P_
                     in_=f_grouped[g][:, cols, :].rearrange("p i t -> p (i t)"),
                 )
 
+        z_planes = [keep.tile([P, PACK, BS], BF16, name="zp%d" % c) for c in range(R_PASSES)]
         z_grouped = [keep.tile([P, BS, PACK], BF16, name="zg%d" % c, align_bytes=64) for c in range(R_PASSES)]
         z_codes = [keep.tile([P, BS], U32, name="zc%d" % c, align_bytes=64) for c in range(R_PASSES)]
         z_scales = [keep.tile([P, BS], U8, name="zs%d" % c, align_bytes=64) for c in range(R_PASSES)]
-        squares = [keep.tile([P, PACK * P], F32, name="sq%d" % ib) for ib in range(ROW_BLOCKS)]
         gram = [gram_pool.tile([P, BS], F32, name="gram%d" % ib) for ib in range(ROW_BLOCKS)]
         col_sums = keep.tile([P, BS], F32)
         n_rows = keep.tile([P, BS], F32)
         n_col = keep.tile([P, ROW_BLOCKS], F32)
-        def project(c, ib):
-            rows = slice(ib * P, (ib + 1) * P)
-            zt = banks.tile([P, PACK, P], F32, tag="bank")
-            for t in range(PACK):
-                for g in range(D_PASSES):
-                    nc.tensor.matmul_mx(
-                        out=zt[:, t, :],
-                        lhsT=p_words[c][:, g, 2 * P * t : 2 * P * (t + 1)].bitcast(FP4X4),
-                        lhsT_scale=p_planes[:, g, c * K_PASS + t * P : c * K_PASS + (t + 1) * P],
-                        rhs=f_codes[g][:, rows].bitcast(FP8X4),
-                        rhs_scale=f_scales[g][:, rows],
-                        start=(g == 0),
-                        stop=(g == D_PASSES - 1),
-                    )
+
+        def project(c, t):
+            zt = banks.tile([P, BS], F32, tag="bank")
+            for g in range(D_PASSES):
+                nc.tensor.matmul_mx(
+                    out=zt[:],
+                    lhsT=p_words[c][:, g, 2 * P * t : 2 * P * (t + 1)].bitcast(FP4X4),
+                    lhsT_scale=p_planes[:, g, c * K_PASS + t * P : c * K_PASS + (t + 1) * P],
+                    rhs=f_codes[g][:].bitcast(FP8X4),
+                    rhs_scale=f_scales[g][:],
+                    start=(g == 0),
+                    stop=(g == D_PASSES - 1),
+                )
             return zt
 
-        def empty_bank(c, ib, zt):
-            rows = slice(ib * P, (ib + 1) * P)
-            fresh = squares[ib] if c == 0 else work.tile([P, PACK * P], F32, name="fresh", tag="fresh")
-            nc.scalar.activation(out=fresh[:], in_=zt[:].rearrange("p t i -> p (t i)"), func=ACT.Square)
-            regrouped = zt[:].rearrange("p t i -> p i t")
-            if ib % 2 == 0:
-                nc.scalar.copy(out=z_grouped[c][:, rows, :], in_=regrouped)
-            else:
-                nc.vector.tensor_copy(out=z_grouped[c][:, rows, :], in_=regrouped)
+        def empty_bank(c, t, zt):
+            first = c == 0 and t == 0
+            fresh = col_sums if first else work.tile([P, BS], F32, name="fresh", tag="fresh")
+            nc.scalar.activation(out=fresh[:], in_=zt[:], func=ACT.Square)
+            nc.scalar.copy(out=z_planes[c][:, t, :], in_=zt[:])
             return fresh
 
-        def quantise_and_add(c, ib, fresh):
-            rows = slice(ib * P, (ib + 1) * P)
-            nc.vector.quantize_mx(
-                out=z_codes[c][:, rows].bitcast(FP8X4),
-                scales=z_scales[c][:, rows],
-                in_=z_grouped[c][:, rows, :].rearrange("p i t -> p (i t)"),
-            )
-            if c > 0:
-                nc.vector.tensor_add(out=squares[ib][:], in0=squares[ib][:], in1=fresh[:])
-            if c == R_PASSES - 1:
-                sq = squares[ib]
-                nc.gpsimd.tensor_tensor(out=sq[:, 0 : 2 * P], in0=sq[:, 0 : 2 * P], in1=sq[:, 2 * P : 4 * P], op=ALU.add)
-                nc.gpsimd.tensor_tensor(out=col_sums[:, rows], in0=sq[:, 0:P], in1=sq[:, P : 2 * P], op=ALU.add)
-
-        def norms(ib):
-            rows = slice(ib * P, (ib + 1) * P)
-            one = slice(ib, ib + 1)
-            nc.tensor.matmul(out=n_rows_ps[:, rows], lhsT=ones[:], rhs=col_sums[:, rows], start=True, stop=True)
-            nc.tensor.matmul(out=n_col_ps[:, one], lhsT=col_sums[:, rows], rhs=ones[:, 0:1], start=True, stop=True)
+        def finish(c, t, fresh):
+            if c > 0 or t > 0:
+                nc.vector.tensor_add(out=col_sums[:], in0=col_sums[:], in1=fresh[:])
+            if t == PACK - 1:
+                nc.vector.tensor_copy(
+                    out=z_grouped[c][:].rearrange("p (b i) t -> p b t i", i=4),
+                    in_=z_planes[c][:].rearrange("p t (b i) -> p b t i", i=4),
+                )
+                nc.vector.quantize_mx(
+                    out=z_codes[c][:].bitcast(FP8X4),
+                    scales=z_scales[c][:],
+                    in_=z_grouped[c][:].rearrange("p i t -> p (i t)"),
+                )
 
         def gram_passes(c):
             for ib in range(ROW_BLOCKS):
@@ -168,20 +157,22 @@ def tile_metric_learning_based_adjacency_matrix_kernel(tc, features, P_words, P_
 
         waiting = None
         for c in range(R_PASSES):
-            for ib in range(ROW_BLOCKS):
-                zt = project(c, ib)
+            for t in range(PACK):
+                zt = project(c, t)
                 if waiting is not None:
-                    quantise_and_add(*waiting)
-                waiting = (c, ib, empty_bank(c, ib, zt))
+                    finish(*waiting)
+                waiting = (c, t, empty_bank(c, t, zt))
             if c > 0:
                 gram_passes(c - 1)
+        finish(*waiting)
         n_rows_ps = banks.tile([P, BS], F32, tag="bank")
         n_col_ps = banks.tile([P, ROW_BLOCKS], F32, tag="bank")
-        quantise_and_add(*waiting)
-        for ib in range(ROW_BLOCKS - 1):
-            norms(ib)
+        nc.tensor.matmul(out=n_rows_ps[:], lhsT=ones[:], rhs=col_sums[:], start=True, stop=True)
+        for ib in range(ROW_BLOCKS):
+            nc.tensor.matmul(
+                out=n_col_ps[:, ib : ib + 1], lhsT=col_sums[:, ib * P : (ib + 1) * P], rhs=ones[:, 0:1], start=True, stop=True
+            )
         gram_passes(R_PASSES - 1)
-        norms(ROW_BLOCKS - 1)
         nc.scalar.copy(out=n_rows[:], in_=n_rows_ps[:])
         nc.vector.tensor_copy(out=n_col[:], in_=n_col_ps[:])
 

@@ -12,14 +12,16 @@ FP8X4 = mybir.dt.float8_e4m3fn_x4
 FP4X4 = mybir.dt.float4_e2m1fn_x4
 ACT = mybir.ActivationFunctionType
 ALU = mybir.AluOpType
+AX = mybir.AxisListType
 
 P = 128
 PACK = 4
 K_PASS = P * PACK
 BS, D, R = 512, 2048, 2048
-ROW_BLOCKS = BS // P
+BLOCKS = BS // P
 D_PASSES = D // K_PASS
-R_PASSES = R // K_PASS
+VECTOR_NORMS = (1,)
+CHUNKS = R // K_PASS
 SQRT_FLOOR = 2.0 ** -116
 
 FLOPS = 2 * BS * D * R + 2 * BS * BS * R
@@ -29,193 +31,289 @@ def tile_metric_learning_based_adjacency_matrix_kernel(tc, features, P_words, P_
     nc = tc.nc
     with ExitStack() as ctx:
         keep = ctx.enter_context(tc.tile_pool(name="keep", bufs=1))
-        work = ctx.enter_context(tc.tile_pool(name="work", bufs=4))
-        banks = ctx.enter_context(tc.psum_pool(name="banks", bufs=4))
-        gram_pool = ctx.enter_context(tc.psum_pool(name="gram", bufs=1))
+        work = ctx.enter_context(tc.tile_pool(name="work", bufs=2))
+        acc_pool = ctx.enter_context(tc.psum_pool(name="acc", bufs=4))
+        flip_pool = ctx.enter_context(tc.psum_pool(name="flip", bufs=4))
         ctx.enter_context(tc.manual_schedule())
 
-        p_planes = keep.tile([P, D_PASSES, R], U8, align_bytes=64)
-        nc.vector.memset(p_planes[:].rearrange("p g n -> p (g n)").bitcast(I32), 0)
+        p_planes = [keep.tile([P, D_PASSES, K_PASS], U8, name="pp%d" % c, align_bytes=64) for c in range(CHUNKS)]
+        for c in range(CHUNKS):
+            nc.vector.memset(p_planes[c][:].rearrange("p g n -> p (g n)").bitcast(I32), 0)
         sqrt_floor = keep.tile([P, 1], F32)
         nc.vector.memset(sqrt_floor[:], SQRT_FLOOR)
-        minus_half = keep.tile([P, 1], F32)
+        minus_half = keep.tile([P, BLOCKS], F32)
         nc.vector.memset(minus_half[:], -0.5)
-        ones = keep.tile([P, P], F32)
-        nc.vector.memset(ones[:], 1.0)
         ident = keep.tile([P, P], F32)
         make_identity(nc, ident[:])
-        off_diag = keep.tile([P, P], F32)
-        nc.vector.tensor_scalar(out=off_diag[:], in0=ident[:], scalar1=-1.0, scalar2=1.0, op0=ALU.mult, op1=ALU.add)
+        off_scale = keep.tile([P, P], F32)
+        nc.vector.tensor_scalar(out=off_scale[:], in0=ident[:], scalar1=-3.0e38, scalar2=0.0, op0=ALU.mult, op1=ALU.add)
         warm = keep.tile([P, 1], F32)
-        nc.scalar.activation(out=warm[:], in_=ones[:, 0:1], func=ACT.Sqrt)
+        nc.scalar.activation(out=warm[:], in_=sqrt_floor[:], func=ACT.Sqrt)
 
-        x_sb = []
-        for ib in range(ROW_BLOCKS):
-            x_blk = keep.tile([P, D], BF16, name="x%d" % ib)
-            nc.sync.dma_start(out=x_blk[:], in_=features[ib * P : (ib + 1) * P, :])
-            x_sb.append(x_blk)
+        zeros = keep.tile([P, BS], BF16)
+        nc.gpsimd.memset(zeros[:], 0.0)
+
+        def warm_up(matmuls):
+            idle = acc_pool.tile([P, BS], F32, name="idle", tag="acc")
+            for k in range(matmuls):
+                nc.tensor.matmul(out=idle[:], lhsT=zeros[:, 0:P], rhs=zeros[:], start=True, stop=True)
+
+        x_sb = [keep.tile([P, D], BF16, name="x%d" % ib) for ib in range(BLOCKS)]
+        p_words = [keep.tile([P, D_PASSES, 2 * K_PASS], U8, name="pw%d" % c, align_bytes=64) for c in range(CHUNKS)]
         scales_i32 = P_scales.bitcast(I32)
         words_i32 = P_words.bitcast(I32)
-        p_words = []
-        for c in range(R_PASSES):
+
+        def load_features(ib, pieces):
+            for s in range(pieces):
+                cols = slice(s * D // pieces, (s + 1) * D // pieces)
+                nc.sync.dma_start(out=x_sb[ib][:, cols], in_=features[ib * P : (ib + 1) * P, cols])
+
+        def load_p(c):
             for q in range(4):
                 nc.sync.dma_start(
-                    out=p_planes[q : P : 32, :, c * K_PASS : (c + 1) * K_PASS].bitcast(I32),
+                    out=p_planes[c][q : P : 32, :, :].bitcast(I32),
                     in_=scales_i32[:, q : 16 : 4, c * (K_PASS // 4) : (c + 1) * (K_PASS // 4)].rearrange("g q n -> q g n"),
                 )
-            chunk = keep.tile([P, D_PASSES, 2 * K_PASS], U8, name="pw%d" % c, align_bytes=64)
             nc.sync.dma_start(
-                out=chunk[:].bitcast(I32),
+                out=p_words[c][:].bitcast(I32),
                 in_=words_i32[:, :, c * (K_PASS // 2) : (c + 1) * (K_PASS // 2)].rearrange("g p w -> p g w"),
             )
-            p_words.append(chunk)
 
-        f_grouped = [keep.tile([P, BS, PACK], BF16, name="fg%d" % g, align_bytes=64) for g in range(D_PASSES)]
-        f_codes = [keep.tile([P, BS], U32, name="fc%d" % g, align_bytes=64) for g in range(D_PASSES)]
-        f_scales = [keep.tile([P, BS], U8, name="fs%d" % g, align_bytes=64) for g in range(D_PASSES)]
-        HALF = BS // 2
-        for h in range(2):
-            flipped = [banks.tile([P, 2, 2, P], F32, name="flip%d" % g, tag="bank") for g in range(D_PASSES)]
-            for j in range(2):
-                x_words = x_sb[2 * h + j][:].bitcast(F32)
-                for g in range(D_PASSES):
-                    for u in range(2):
-                        nc.tensor.transpose(
-                            flipped[g][:, u, j, :], x_words[:, 256 * g + u : 256 * (g + 1) : 2], ident[:]
-                        )
-            cols = slice(h * HALF, (h + 1) * HALF)
-            for g in range(D_PASSES):
-                pairs = f_grouped[g][:].rearrange("p i t -> p (i t)").bitcast(F32).rearrange("p (i u) -> p i u", u=2)
-                source = flipped[g][:].rearrange("p u j i -> p (j i) u")
-                if g % 2 == 0:
-                    nc.vector.tensor_copy(out=pairs[:, cols, :], in_=source)
-                else:
-                    nc.scalar.copy(out=pairs[:, cols, :], in_=source)
-            for g in range(D_PASSES):
-                nc.vector.quantize_mx(
-                    out=f_codes[g][:, cols].bitcast(FP8X4),
-                    scales=f_scales[g][:, cols],
-                    in_=f_grouped[g][:, cols, :].rearrange("p i t -> p (i t)"),
-                )
+        load_features(0, 4)
+        load_p(0)
+        load_features(1, 1)
+        load_p(1)
+        load_p(2)
+        load_p(3)
+        load_features(2, 1)
+        load_features(3, 1)
 
-        z_planes = [keep.tile([P, PACK, BS], BF16, name="zp%d" % c) for c in range(R_PASSES)]
-        z_grouped = [keep.tile([P, BS, PACK], BF16, name="zg%d" % c, align_bytes=64) for c in range(R_PASSES)]
-        z_codes = [keep.tile([P, BS], U32, name="zc%d" % c, align_bytes=64) for c in range(R_PASSES)]
-        z_scales = [keep.tile([P, BS], U8, name="zs%d" % c, align_bytes=64) for c in range(R_PASSES)]
-        gram = [gram_pool.tile([P, BS], F32, name="gram%d" % ib) for ib in range(ROW_BLOCKS)]
-        col_sums = keep.tile([P, BS], F32)
+        f_grouped = [keep.tile([P, D_PASSES, P, PACK], BF16, name="fg%d" % ib, align_bytes=64) for ib in range(BLOCKS)]
+        f_codes = [keep.tile([P, D_PASSES, P], U32, name="fc%d" % ib, align_bytes=64) for ib in range(BLOCKS)]
+        f_scales = [keep.tile([P, D_PASSES, P], U8, name="fs%d" % ib, align_bytes=64) for ib in range(BLOCKS)]
+        z_rows = [keep.tile([P, R], BF16, name="zr%d" % ib, align_bytes=64) for ib in range(BLOCKS)]
+        z_codes = [keep.tile([P, BS], U32, name="zc%d" % c, align_bytes=64) for c in range(CHUNKS)]
+        z_scales = [keep.tile([P, BS], U8, name="zs%d" % c, align_bytes=64) for c in range(CHUNKS)]
+        n_parts = keep.tile([P, BLOCKS, CHUNKS], F32)
+        stats = {ib: keep.tile([P, CHUNKS, 6], F32, name="st%d" % ib) for ib in VECTOR_NORMS}
+        n_col = keep.tile([P, BLOCKS], F32)
         n_rows = keep.tile([P, BS], F32)
-        n_col = keep.tile([P, ROW_BLOCKS], F32)
+        n_diag = keep.tile([P, BS], F32)
 
-        def project(c, t):
-            zt = banks.tile([P, BS], F32, tag="bank")
+        def flip_features(ib):
+            words = x_sb[ib][:].bitcast(F32)
+            jobs = []
+            for h in range(2):
+                bank = flip_pool.tile([P, 2, 2, P], F32, name="xbank", tag="flip")
+                for a in range(2):
+                    g = 2 * h + a
+                    for u in range(2):
+                        nc.tensor.transpose(bank[:, a, u, :], words[:, 256 * g + u : 256 * (g + 1) : 2], ident[:])
+                half = slice(2 * h, 2 * h + 2)
+                codes = f_codes[ib][:, half].rearrange("p g i -> p (g i)")
+                scales = f_scales[ib][:, half].rearrange("p g i -> p (g i)")
+                grouped = f_grouped[ib][:, half]
+                jobs.append((bank[:], grouped, [(codes, scales, grouped.rearrange("p g i t -> p (g i t)"))]))
+            return jobs
+
+        def flip_z(ib, chunks):
+            words = z_rows[ib][:].bitcast(F32)
+            bank = flip_pool.tile([P, 2, 2, P], F32, name="zbank", tag="flip")
+            grouped = work.tile([P, 2, P, PACK], BF16, name="zg", tag="zg", bufs=4, align_bytes=64)
+            rows = slice(ib * P, (ib + 1) * P)
+            quants = []
+            for a, c in enumerate(chunks):
+                for u in range(2):
+                    nc.tensor.transpose(bank[:, a, u, :], words[:, 256 * c + P * u : 256 * c + P * (u + 1)], ident[:])
+                quants.append((z_codes[c][:, rows], z_scales[c][:, rows], grouped[:, a].rearrange("p i t -> p (i t)")))
+            n = len(chunks)
+            return [(bank[:, 0:n], grouped[:, 0:n], quants)]
+
+        def unload(jobs, scalar=()):
+            for k, (bank, grouped, quants) in enumerate(jobs):
+                target = grouped.rearrange("p a i t -> p (a i t)").bitcast(F32).rearrange("p (a i u) -> p a i u", u=2, i=P)
+                source = bank.rearrange("p a u i -> p a i u")
+                if k in scalar:
+                    nc.scalar.copy(out=target, in_=source)
+                else:
+                    nc.vector.tensor_copy(out=target, in_=source)
+
+        def quantise(jobs):
+            for bank, grouped, quants in jobs:
+                for codes, scales, values in quants:
+                    nc.vector.quantize_mx(out=codes.bitcast(FP8X4), scales=scales, in_=values)
+
+        def project(ib, c):
+            zt = acc_pool.tile([P, BS], F32, name="zt", tag="acc")
             for g in range(D_PASSES):
                 nc.tensor.matmul_mx(
                     out=zt[:],
-                    lhsT=p_words[c][:, g, 2 * P * t : 2 * P * (t + 1)].bitcast(FP4X4),
-                    lhsT_scale=p_planes[:, g, c * K_PASS + t * P : c * K_PASS + (t + 1) * P],
-                    rhs=f_codes[g][:].bitcast(FP8X4),
-                    rhs_scale=f_scales[g][:],
+                    lhsT=f_codes[ib][:, g, :].bitcast(FP8X4),
+                    lhsT_scale=f_scales[ib][:, g, :],
+                    rhs=p_words[c][:, g, :].bitcast(FP4X4),
+                    rhs_scale=p_planes[c][:, g, :],
                     start=(g == 0),
                     stop=(g == D_PASSES - 1),
                 )
-            return zt
+            nc.scalar.copy(
+                out=z_rows[ib][:, c * K_PASS : (c + 1) * K_PASS].rearrange("i (u p e) -> i u p e", u=2, e=2),
+                in_=zt[:].rearrange("i (p u e) -> i u p e", u=2, e=2),
+            )
+            if ib in VECTOR_NORMS:
+                nc.vector.bn_stats(out=stats[ib][:, c, :], in_=zt[:])
+            else:
+                squares = work.tile([P, BS], F32, name="squares", tag="squares")
+                nc.scalar.activation(out=squares[:], in_=zt[:], func=ACT.Square, accum_out=n_parts[:, ib, c : c + 1])
 
-        def empty_bank(c, t, zt):
-            first = c == 0 and t == 0
-            fresh = col_sums if first else work.tile([P, BS], F32, name="fresh", tag="fresh")
-            nc.scalar.activation(out=fresh[:], in_=zt[:], func=ACT.Square)
-            nc.scalar.copy(out=z_planes[c][:, t, :], in_=zt[:])
-            return fresh
+        def norm_columns(blocks):
+            for ib in blocks:
+                one = n_col[:, ib : ib + 1]
+                if ib in VECTOR_NORMS:
+                    moments = work.tile([P, 2], F32, name="moments", tag="moments")
+                    nc.vector.bn_aggr(out=moments[:], in_=stats[ib][:].rearrange("p c s -> p (c s)"))
+                    nc.vector.scalar_tensor_tensor(
+                        out=one, in0=moments[:, 0:1], scalar=moments[:, 0:1], in1=moments[:, 1:2], op0=ALU.mult, op1=ALU.add
+                    )
+                    nc.vector.tensor_scalar(out=one, in0=one, scalar1=float(R), scalar2=0.0, op0=ALU.mult, op1=ALU.add)
+                else:
+                    nc.vector.tensor_reduce(out=one, in_=n_parts[:, ib, :], op=ALU.add, axis=AX.X)
 
-        def finish(c, t, fresh):
-            if c > 0 or t > 0:
-                nc.vector.tensor_add(out=col_sums[:], in0=col_sums[:], in1=fresh[:])
-            if t == PACK - 1:
-                nc.vector.tensor_copy(
-                    out=z_grouped[c][:].rearrange("p (b i) t -> p b t i", i=4),
-                    in_=z_planes[c][:].rearrange("p t (b i) -> p b t i", i=4),
-                )
-                nc.vector.quantize_mx(
-                    out=z_codes[c][:].bitcast(FP8X4),
-                    scales=z_scales[c][:],
-                    in_=z_grouped[c][:].rearrange("p i t -> p (i t)"),
-                )
+        def norm_rows(blocks):
+            spread = acc_pool.tile([P, BS], F32, name="spread", tag="acc")
+            for ib in blocks:
+                own = slice(ib * P, (ib + 1) * P)
+                nc.tensor.transpose(spread[:, own], n_col[:, ib : ib + 1].to_broadcast([P, P]), ident[:])
+            for ib in blocks:
+                own = slice(ib * P, (ib + 1) * P)
+                nc.vector.tensor_add(out=n_diag[:, own], in0=spread[:, own], in1=off_scale[:])
+            some = slice(blocks[0] * P, (blocks[-1] + 1) * P)
+            if blocks[-1] < BLOCKS - 1:
+                nc.vector.tensor_copy(out=n_rows[:, some], in_=spread[:, some])
 
-        def gram_passes(c):
-            for ib in range(ROW_BLOCKS):
-                rows = slice(ib * P, (ib + 1) * P)
+        dist = keep.tile([P, BLOCKS, BS], F32)
+        gram_of = {}
+
+        def gram(ib, chunks, lo=0, hi=None):
+            hi = (ib + 1) * P if hi is None else hi
+            if ib not in gram_of:
+                gram_of[ib] = acc_pool.tile([P, BS], F32, name="gram", tag="acc")
+            rows = slice(ib * P, (ib + 1) * P)
+            for c in chunks:
                 nc.tensor.matmul_mx(
-                    out=gram[ib][:],
+                    out=gram_of[ib][:, lo:hi],
                     lhsT=z_codes[c][:, rows].bitcast(FP8X4),
                     lhsT_scale=z_scales[c][:, rows],
-                    rhs=z_codes[c][:].bitcast(FP8X4),
-                    rhs_scale=z_scales[c][:],
+                    rhs=z_codes[c][:, lo:hi].bitcast(FP8X4),
+                    rhs_scale=z_scales[c][:, lo:hi],
                     start=(c == 0),
-                    stop=(c == R_PASSES - 1),
+                    stop=(c == CHUNKS - 1),
                 )
 
-        waiting = None
-        for c in range(R_PASSES):
-            for t in range(PACK):
-                zt = project(c, t)
-                if waiting is not None:
-                    finish(*waiting)
-                waiting = (c, t, empty_bank(c, t, zt))
-            if c > 0:
-                gram_passes(c - 1)
-        finish(*waiting)
-        n_rows_ps = banks.tile([P, BS], F32, tag="bank")
-        n_col_ps = banks.tile([P, ROW_BLOCKS], F32, tag="bank")
-        nc.tensor.matmul(out=n_rows_ps[:], lhsT=ones[:], rhs=col_sums[:], start=True, stop=True)
-        for ib in range(ROW_BLOCKS):
-            nc.tensor.matmul(
-                out=n_col_ps[:, ib : ib + 1], lhsT=col_sums[:, ib * P : (ib + 1) * P], rhs=ones[:, 0:1], start=True, stop=True
-            )
-        gram_passes(R_PASSES - 1)
-        nc.scalar.copy(out=n_rows[:], in_=n_rows_ps[:])
-        nc.vector.tensor_copy(out=n_col[:], in_=n_col_ps[:])
+        def distances(ib, pieces):
+            own = ib * P
+            for lo, hi in pieces:
+                sq = work.tile([P, BS], F32, name="sq", tag="sq", bufs=3)
+                for a, b, row in ((lo, min(hi, own), n_rows), (max(lo, own), hi, n_diag)):
+                    if a < b:
+                        nc.vector.scalar_tensor_tensor(
+                            out=sq[:, a:b], in0=gram_of[ib][:, a:b], scalar=-2.0, in1=row[:, a:b], op0=ALU.mult, op1=ALU.add
+                        )
+                nc.vector.tensor_scalar(
+                    out=sq[:, lo:hi], in0=sq[:, lo:hi], scalar1=n_col[:, ib : ib + 1], scalar2=0.0, op0=ALU.add, op1=ALU.max
+                )
+                nc.scalar.activation(out=dist[:, ib, lo:hi], in_=sq[:, lo:hi], func=ACT.Sqrt, bias=sqrt_floor[:])
 
-        dist = [keep.tile([P, BS], F32, name="dist%d" % ib) for ib in range(ROW_BLOCKS)]
-        for ib in range(ROW_BLOCKS):
-            rows = slice(ib * P, (ib + 1) * P)
-            sq_dist = work.tile([P, BS], F32, tag="sq_dist")
-            nc.vector.scalar_tensor_tensor(
-                out=sq_dist[:], in0=gram[ib][:], scalar=-2.0, in1=n_rows[:], op0=ALU.mult, op1=ALU.add
-            )
-            nc.vector.tensor_scalar(
-                out=sq_dist[:], in0=sq_dist[:], scalar1=n_col[:, ib : ib + 1], scalar2=0.0, op0=ALU.add, op1=ALU.max
-            )
-            nc.scalar.activation(out=dist[ib][:], in_=sq_dist[:], func=ACT.Sqrt, bias=sqrt_floor[:])
-        for ib in range(ROW_BLOCKS):
-            rows = slice(ib * P, (ib + 1) * P)
-            nc.vector.tensor_mul(out=dist[ib][:, rows], in0=dist[ib][:, rows], in1=off_diag[:])
+        def mirror(ib, lo=0, hi=None):
+            hi = ib if hi is None else hi
+            own = slice(ib * P, (ib + 1) * P)
+            mirrored = flip_pool.tile([P, BLOCKS, P], F32, name="mirrored", tag="flip")
+            for jb in range(lo, hi):
+                nc.tensor.transpose(mirrored[:, jb, :], dist[:, ib, jb * P : (jb + 1) * P], ident[:])
+            nc.vector.tensor_copy(out=dist[:, lo:hi, own], in_=mirrored[:, lo:hi, :])
 
-        adj = [keep.tile([P, BS], F32, name="adj%d" % ib) for ib in range(ROW_BLOCKS)]
-        deg = keep.tile([P, ROW_BLOCKS], F32)
-        inv_sqrt_deg = keep.tile([P, ROW_BLOCKS], F32)
-        inv_rows_ps = banks.tile([P, BS], F32, tag="bank")
-        for ib in range(ROW_BLOCKS):
-            rows = slice(ib * P, (ib + 1) * P)
+        every = range(CHUNKS)
+        warm_up(3)
+        f0 = flip_features(0)
+        warm_up(2)
+        unload(f0, scalar=(1,))
+        quantise(f0)
+        project(0, 0)
+        f1 = flip_features(1)
+        unload(f1)
+        quantise(f1)
+        project(0, 1)
+        project(1, 0)
+        project(1, 1)
+        project(0, 2)
+        project(0, 3)
+        f2 = flip_features(2) + flip_z(0, (0, 1)) + flip_z(1, (0, 1))
+        unload(f2)
+        quantise(f2)
+        project(1, 2)
+        project(1, 3)
+        project(2, 0)
+        project(2, 1)
+        norm_columns([0, 1])
+        f3 = flip_features(3) + flip_z(0, (2, 3)) + flip_z(1, (2, 3))
+        unload(f3)
+        norm_rows([0, 1])
+        quantise(f3)
+        project(2, 2)
+        project(2, 3)
+        project(3, 0)
+        gram(0, every)
+        gram(1, every)
+        distances(0, [(0, 128)])
+        distances(1, [(0, 256)])
+        project(3, 1)
+        norm_columns([2])
+        z2 = flip_z(2, (0, 1)) + flip_z(2, (2, 3))
+        unload(z2)
+        quantise(z2)
+        norm_rows([2])
+        mirror(1)
+        project(3, 2)
+        z3 = flip_z(3, (0, 1))
+        unload(z3)
+        quantise(z3)
+        project(3, 3)
+        z3 = flip_z(3, (2,))
+        unload(z3)
+        quantise(z3)
+        gram(2, every, 0, 256)
+        distances(2, [(0, 256)])
+        z3 = flip_z(3, (3,))
+        unload(z3)
+        norm_columns([3])
+        quantise(z3)
+        gram(2, every, 256, 384)
+        gram(3, (0, 1, 2))
+        norm_rows([3])
+        gram(3, (3,))
+        distances(2, [(256, 384)])
+        distances(3, [(0, 256), (256, 512)])
+        mirror(2)
+        mirror(3, 0, 2)
+        mirror(3, 2, 3)
+
+        adj = [keep.tile([P, BS], F32, name="adj%d" % ib) for ib in range(BLOCKS)]
+        deg = keep.tile([P, BLOCKS], F32)
+        inv_sqrt_deg = keep.tile([P, BLOCKS], F32)
+        inv_rows = flip_pool.tile([P, BS], F32, name="inv_rows", tag="flip")
+        for ib in reversed(range(BLOCKS)):
             one = slice(ib, ib + 1)
-            nc.scalar.activation(out=adj[ib][:], in_=dist[ib][:], func=ACT.Exp, scale=-1.0, accum_out=deg[:, one])
-            nc.vector.scalar_tensor_tensor(
-                out=adj[ib][:, rows], in0=adj[ib][:, rows], scalar=1.0, in1=ident[:], op0=ALU.min, op1=ALU.max
-            )
-            nc.sync.dma_start(out=out_1[rows, :], in_=adj[ib][:])
-            nc.gpsimd.tensor_tensor(out=inv_sqrt_deg[:, one], in0=deg[:, one], in1=minus_half[:], op=ALU.pow)
-            nc.tensor.matmul(
-                out=inv_rows_ps[:, rows], lhsT=inv_sqrt_deg[:, one].to_broadcast([P, P]), rhs=ident[:], start=True, stop=True
-            )
-        for ib in range(ROW_BLOCKS):
-            rows = slice(ib * P, (ib + 1) * P)
-            normalized = work.tile([P, BS], F32, tag="normalized")
+            nc.scalar.activation(out=adj[ib][:], in_=dist[:, ib, :], func=ACT.Exp, scale=-1.0, accum_out=deg[:, one])
+            nc.sync.dma_start(out=out_1[ib * P : (ib + 1) * P, :], in_=adj[ib][:])
+            nc.gpsimd.tensor_tensor(out=inv_sqrt_deg[:, one], in0=deg[:, one], in1=minus_half[:, one], op=ALU.pow)
+            nc.tensor.transpose(inv_rows[:, ib * P : (ib + 1) * P], inv_sqrt_deg[:, one].to_broadcast([P, P]), ident[:])
+        for ib in reversed(range(BLOCKS)):
+            normalized = work.tile([P, BS], F32, name="normalized", tag="normalized", bufs=4)
             nc.vector.scalar_tensor_tensor(
                 out=normalized[:],
                 in0=adj[ib][:],
                 scalar=inv_sqrt_deg[:, ib : ib + 1],
-                in1=inv_rows_ps[:],
+                in1=inv_rows[:],
                 op0=ALU.mult,
                 op1=ALU.mult,
             )
-            nc.sync.dma_start(out=out_0[rows, :], in_=normalized[:])
+            nc.sync.dma_start(out=out_0[ib * P : (ib + 1) * P, :], in_=normalized[:])

@@ -36,9 +36,9 @@ def tile_metric_learning_based_adjacency_matrix_kernel(tc, features, P_words, P_
         flip_pool = ctx.enter_context(tc.psum_pool(name="flip", bufs=4))
         ctx.enter_context(tc.manual_schedule())
 
-        p_planes = [keep.tile([P, D_PASSES, K_PASS], U8, name="pp%d" % c, align_bytes=64) for c in range(CHUNKS)]
-        for c in range(CHUNKS):
-            nc.vector.memset(p_planes[c][:].rearrange("p g n -> p (g n)").bitcast(I32), 0)
+        p_planes = [keep.tile([P, D_PASSES, 2 * K_PASS], U8, name="pp%d" % h, align_bytes=64) for h in range(CHUNKS // 2)]
+        for h in range(CHUNKS // 2):
+            nc.vector.memset(p_planes[h][:].rearrange("p g n -> p (g n)").bitcast(I32), 0)
         sqrt_floor = keep.tile([P, 1], F32)
         nc.vector.memset(sqrt_floor[:], SQRT_FLOOR)
         minus_half = keep.tile([P, BLOCKS], F32)
@@ -68,21 +68,25 @@ def tile_metric_learning_based_adjacency_matrix_kernel(tc, features, P_words, P_
                 cols = slice(s * D // pieces, (s + 1) * D // pieces)
                 nc.sync.dma_start(out=x_sb[ib][:, cols], in_=features[ib * P : (ib + 1) * P, cols])
 
-        def load_p(c):
+        def load_scales(h):
             for q in range(4):
                 nc.sync.dma_start(
-                    out=p_planes[c][q : P : 32, :, :].bitcast(I32),
-                    in_=scales_i32[:, q : 16 : 4, c * (K_PASS // 4) : (c + 1) * (K_PASS // 4)].rearrange("g q n -> q g n"),
+                    out=p_planes[h][q : P : 32, :, :].bitcast(I32),
+                    in_=scales_i32[:, q : 16 : 4, h * (K_PASS // 2) : (h + 1) * (K_PASS // 2)].rearrange("g q n -> q g n"),
                 )
+
+        def load_p(c):
             nc.sync.dma_start(
                 out=p_words[c][:].bitcast(I32),
                 in_=words_i32[:, :, c * (K_PASS // 2) : (c + 1) * (K_PASS // 2)].rearrange("g p w -> p g w"),
             )
 
-        load_features(0, 4)
+        load_features(0, 2)
+        load_scales(0)
         load_p(0)
         load_features(1, 1)
         load_p(1)
+        load_scales(1)
         load_p(2)
         load_p(3)
         load_features(2, 1)
@@ -151,7 +155,7 @@ def tile_metric_learning_based_adjacency_matrix_kernel(tc, features, P_words, P_
                     lhsT=f_codes[ib][:, g, :].bitcast(FP8X4),
                     lhsT_scale=f_scales[ib][:, g, :],
                     rhs=p_words[c][:, g, :].bitcast(FP4X4),
-                    rhs_scale=p_planes[c][:, g, :],
+                    rhs_scale=p_planes[c // 2][:, g, (c % 2) * K_PASS : (c % 2 + 1) * K_PASS],
                     start=(g == 0),
                     stop=(g == D_PASSES - 1),
                 )
@@ -188,7 +192,7 @@ def tile_metric_learning_based_adjacency_matrix_kernel(tc, features, P_words, P_
                 nc.vector.tensor_add(out=n_diag[:, own], in0=spread[:, own], in1=off_scale[:])
             some = slice(blocks[0] * P, (blocks[-1] + 1) * P)
             if blocks[-1] < BLOCKS - 1:
-                nc.vector.tensor_copy(out=n_rows[:, some], in_=spread[:, some])
+                nc.scalar.copy(out=n_rows[:, some], in_=spread[:, some])
 
         dist = keep.tile([P, BLOCKS, BS], F32)
         gram_of = {}
@@ -209,19 +213,33 @@ def tile_metric_learning_based_adjacency_matrix_kernel(tc, features, P_words, P_
                     stop=(c == CHUNKS - 1),
                 )
 
-        def distances(ib, pieces):
+        def squared(ib, lo, hi):
             own = ib * P
-            for lo, hi in pieces:
-                sq = work.tile([P, BS], F32, name="sq", tag="sq", bufs=3)
-                for a, b, row in ((lo, min(hi, own), n_rows), (max(lo, own), hi, n_diag)):
-                    if a < b:
-                        nc.vector.scalar_tensor_tensor(
-                            out=sq[:, a:b], in0=gram_of[ib][:, a:b], scalar=-2.0, in1=row[:, a:b], op0=ALU.mult, op1=ALU.add
-                        )
+            sq = work.tile([P, BS], F32, name="sq", tag="sq", bufs=4)
+            for a, b, row in ((lo, min(hi, own), n_rows), (max(lo, own), hi, n_diag)):
+                if a < b:
+                    nc.vector.scalar_tensor_tensor(
+                        out=sq[:, a:b], in0=gram_of[ib][:, a:b], scalar=-2.0, in1=row[:, a:b], op0=ALU.mult, op1=ALU.add
+                    )
+            return ib, lo, hi, sq
+
+        def rooted(ib, lo, hi, sq):
+            if ib == 2:
+                nc.scalar.activation(out=sq[:, lo:hi], in_=sq[:, lo:hi], func=ACT.Relu, bias=n_col[:, ib : ib + 1])
+            else:
                 nc.vector.tensor_scalar(
                     out=sq[:, lo:hi], in0=sq[:, lo:hi], scalar1=n_col[:, ib : ib + 1], scalar2=0.0, op0=ALU.add, op1=ALU.max
                 )
-                nc.scalar.activation(out=dist[:, ib, lo:hi], in_=sq[:, lo:hi], func=ACT.Sqrt, bias=sqrt_floor[:])
+            nc.scalar.activation(out=dist[:, ib, lo:hi], in_=sq[:, lo:hi], func=ACT.Sqrt, bias=sqrt_floor[:])
+
+        def distances(pieces):
+            before = None
+            for piece in pieces:
+                now = squared(*piece)
+                if before is not None:
+                    rooted(*before)
+                before = now
+            rooted(*before)
 
         def mirror(ib, lo=0, hi=None):
             hi = ib if hi is None else hi
@@ -263,35 +281,37 @@ def tile_metric_learning_based_adjacency_matrix_kernel(tc, features, P_words, P_
         project(3, 0)
         gram(0, every)
         gram(1, every)
-        distances(0, [(0, 128)])
-        distances(1, [(0, 256)])
+        distances([(0, 0, 128), (1, 0, 256)])
         project(3, 1)
         norm_columns([2])
         z2 = flip_z(2, (0, 1)) + flip_z(2, (2, 3))
         unload(z2)
         quantise(z2)
         norm_rows([2])
-        mirror(1)
         project(3, 2)
         z3 = flip_z(3, (0, 1))
         unload(z3)
         quantise(z3)
         project(3, 3)
         z3 = flip_z(3, (2,))
-        unload(z3)
-        quantise(z3)
         gram(2, every, 0, 256)
-        distances(2, [(0, 256)])
+        unload(z3)
+        near = squared(2, 0, 256)
+        quantise(z3)
         z3 = flip_z(3, (3,))
+        rooted(*near)
         unload(z3)
         norm_columns([3])
         quantise(z3)
         gram(2, every, 256, 384)
-        gram(3, (0, 1, 2))
+        gram(3, every)
+        own_2 = squared(2, 256, 384)
+        others_3 = squared(3, 0, 384)
         norm_rows([3])
-        gram(3, (3,))
-        distances(2, [(256, 384)])
-        distances(3, [(0, 256), (256, 512)])
+        rooted(*own_2)
+        rooted(*others_3)
+        distances([(3, 384, 512)])
+        mirror(1)
         mirror(2)
         mirror(3, 0, 2)
         mirror(3, 2, 3)
@@ -299,21 +319,32 @@ def tile_metric_learning_based_adjacency_matrix_kernel(tc, features, P_words, P_
         adj = [keep.tile([P, BS], F32, name="adj%d" % ib) for ib in range(BLOCKS)]
         deg = keep.tile([P, BLOCKS], F32)
         inv_sqrt_deg = keep.tile([P, BLOCKS], F32)
-        inv_rows = flip_pool.tile([P, BS], F32, name="inv_rows", tag="flip")
-        for ib in reversed(range(BLOCKS)):
-            one = slice(ib, ib + 1)
-            nc.scalar.activation(out=adj[ib][:], in_=dist[:, ib, :], func=ACT.Exp, scale=-1.0, accum_out=deg[:, one])
-            nc.sync.dma_start(out=out_1[ib * P : (ib + 1) * P, :], in_=adj[ib][:])
-            nc.gpsimd.tensor_tensor(out=inv_sqrt_deg[:, one], in0=deg[:, one], in1=minus_half[:, one], op=ALU.pow)
-            nc.tensor.transpose(inv_rows[:, ib * P : (ib + 1) * P], inv_sqrt_deg[:, one].to_broadcast([P, P]), ident[:])
-        for ib in reversed(range(BLOCKS)):
-            normalized = work.tile([P, BS], F32, name="normalized", tag="normalized", bufs=4)
+        normalized = [keep.tile([P, BS], F32, name="normalized%d" % ib) for ib in range(BLOCKS)]
+        halves = (slice(0, BS // 2), slice(BS // 2, BS))
+        inv_rows = {}
+
+        def normalise(ib, half):
+            cols = halves[half]
             nc.vector.scalar_tensor_tensor(
-                out=normalized[:],
-                in0=adj[ib][:],
+                out=normalized[ib][:, cols],
+                in0=adj[ib][:, cols],
                 scalar=inv_sqrt_deg[:, ib : ib + 1],
-                in1=inv_rows[:],
+                in1=inv_rows[half][:],
                 op0=ALU.mult,
                 op1=ALU.mult,
             )
-            nc.sync.dma_start(out=out_0[ib * P : (ib + 1) * P, :], in_=normalized[:])
+            nc.sync.dma_start(out=out_0[ib * P : (ib + 1) * P, cols], in_=normalized[ib][:, cols])
+
+        for half in (1, 0):
+            inv_rows[half] = flip_pool.tile([P, BS // 2], F32, name="inv_rows", tag="flip")
+            for side in (1, 0):
+                ib = 2 * half + side
+                one = slice(ib, ib + 1)
+                nc.scalar.activation(out=adj[ib][:], in_=dist[:, ib, :], func=ACT.Exp, scale=-1.0, accum_out=deg[:, one])
+                nc.sync.dma_start(out=out_1[ib * P : (ib + 1) * P, :], in_=adj[ib][:])
+                nc.gpsimd.tensor_tensor(out=inv_sqrt_deg[:, one], in0=deg[:, one], in1=minus_half[:, one], op=ALU.pow)
+                nc.tensor.transpose(
+                    inv_rows[half][:, side * P : (side + 1) * P], inv_sqrt_deg[:, one].to_broadcast([P, P]), ident[:]
+                )
+        for ib, half in ((3, 1), (2, 1), (3, 0), (2, 0), (1, 1), (1, 0), (0, 1), (0, 0)):
+            normalise(ib, half)

@@ -36,9 +36,9 @@ def tile_metric_learning_based_adjacency_matrix_kernel(tc, features, P_words, P_
         flip_pool = ctx.enter_context(tc.psum_pool(name="flip", bufs=4))
         ctx.enter_context(tc.manual_schedule())
 
-        p_planes = [keep.tile([P, D_PASSES, 2 * K_PASS], U8, name="pp%d" % h, align_bytes=64) for h in range(CHUNKS // 2)]
-        for h in range(CHUNKS // 2):
-            nc.vector.memset(p_planes[h][:].rearrange("p g n -> p (g n)").bitcast(I32), 0)
+        p_planes = [keep.tile([P, D_PASSES, K_PASS], U8, name="pp%d" % c, align_bytes=64) for c in range(CHUNKS)]
+        for c in range(CHUNKS):
+            nc.vector.memset(p_planes[c][:].rearrange("p g n -> p (g n)").bitcast(I32), 0)
         sqrt_floor = keep.tile([P, 1], F32)
         nc.vector.memset(sqrt_floor[:], SQRT_FLOOR)
         minus_half = keep.tile([P, BLOCKS], F32)
@@ -68,25 +68,21 @@ def tile_metric_learning_based_adjacency_matrix_kernel(tc, features, P_words, P_
                 cols = slice(s * D // pieces, (s + 1) * D // pieces)
                 nc.sync.dma_start(out=x_sb[ib][:, cols], in_=features[ib * P : (ib + 1) * P, cols])
 
-        def load_scales(h):
+        def load_p(c):
             for q in range(4):
                 nc.sync.dma_start(
-                    out=p_planes[h][q : P : 32, :, :].bitcast(I32),
-                    in_=scales_i32[:, q : 16 : 4, h * (K_PASS // 2) : (h + 1) * (K_PASS // 2)].rearrange("g q n -> q g n"),
+                    out=p_planes[c][q : P : 32, :, :].bitcast(I32),
+                    in_=scales_i32[:, q : 16 : 4, c * (K_PASS // 4) : (c + 1) * (K_PASS // 4)].rearrange("g q n -> q g n"),
                 )
-
-        def load_p(c):
             nc.sync.dma_start(
                 out=p_words[c][:].bitcast(I32),
                 in_=words_i32[:, :, c * (K_PASS // 2) : (c + 1) * (K_PASS // 2)].rearrange("g p w -> p g w"),
             )
 
         load_features(0, 2)
-        load_scales(0)
         load_p(0)
         load_features(1, 1)
         load_p(1)
-        load_scales(1)
         load_p(2)
         load_p(3)
         load_features(2, 1)
@@ -155,7 +151,7 @@ def tile_metric_learning_based_adjacency_matrix_kernel(tc, features, P_words, P_
                     lhsT=f_codes[ib][:, g, :].bitcast(FP8X4),
                     lhsT_scale=f_scales[ib][:, g, :],
                     rhs=p_words[c][:, g, :].bitcast(FP4X4),
-                    rhs_scale=p_planes[c // 2][:, g, (c % 2) * K_PASS : (c % 2 + 1) * K_PASS],
+                    rhs_scale=p_planes[c][:, g, :],
                     start=(g == 0),
                     stop=(g == D_PASSES - 1),
                 )
@@ -182,7 +178,7 @@ def tile_metric_learning_based_adjacency_matrix_kernel(tc, features, P_words, P_
                 else:
                     nc.vector.tensor_reduce(out=one, in_=n_parts[:, ib, :], op=ALU.add, axis=AX.X)
 
-        def norm_rows(blocks):
+        def norm_rows(blocks, copy):
             spread = acc_pool.tile([P, BS], F32, name="spread", tag="acc")
             for ib in blocks:
                 own = slice(ib * P, (ib + 1) * P)
@@ -192,7 +188,7 @@ def tile_metric_learning_based_adjacency_matrix_kernel(tc, features, P_words, P_
                 nc.vector.tensor_add(out=n_diag[:, own], in0=spread[:, own], in1=off_scale[:])
             some = slice(blocks[0] * P, (blocks[-1] + 1) * P)
             if blocks[-1] < BLOCKS - 1:
-                nc.scalar.copy(out=n_rows[:, some], in_=spread[:, some])
+                copy(out=n_rows[:, some], in_=spread[:, some])
 
         dist = keep.tile([P, BLOCKS, BS], F32)
         gram_of = {}
@@ -274,7 +270,7 @@ def tile_metric_learning_based_adjacency_matrix_kernel(tc, features, P_words, P_
         norm_columns([0, 1])
         f3 = flip_features(3) + flip_z(0, (2, 3)) + flip_z(1, (2, 3))
         unload(f3)
-        norm_rows([0, 1])
+        norm_rows([0, 1], nc.vector.tensor_copy)
         quantise(f3)
         project(2, 2)
         project(2, 3)
@@ -287,7 +283,7 @@ def tile_metric_learning_based_adjacency_matrix_kernel(tc, features, P_words, P_
         z2 = flip_z(2, (0, 1)) + flip_z(2, (2, 3))
         unload(z2)
         quantise(z2)
-        norm_rows([2])
+        norm_rows([2], nc.scalar.copy)
         project(3, 2)
         z3 = flip_z(3, (0, 1))
         unload(z3)
@@ -304,47 +300,101 @@ def tile_metric_learning_based_adjacency_matrix_kernel(tc, features, P_words, P_
         norm_columns([3])
         quantise(z3)
         gram(2, every, 256, 384)
-        gram(3, every)
+        gram(3, (0, 1, 2))
         own_2 = squared(2, 256, 384)
+        norm_rows([3], None)
+        gram(3, (3,))
         others_3 = squared(3, 0, 384)
-        norm_rows([3])
         rooted(*own_2)
+        own_3 = squared(3, 384, 512)
         rooted(*others_3)
-        distances([(3, 384, 512)])
+        rooted(*own_3)
         mirror(1)
         mirror(2)
         mirror(3, 0, 2)
         mirror(3, 2, 3)
 
-        adj = [keep.tile([P, BS], F32, name="adj%d" % ib) for ib in range(BLOCKS)]
+        adj = keep.tile([P, BLOCKS, BS], F32)
+        normalized = keep.tile([P, BLOCKS, BS], F32)
+        scaled = keep.tile([P, BLOCKS, BS // 2], F32)
         deg = keep.tile([P, BLOCKS], F32)
         inv_sqrt_deg = keep.tile([P, BLOCKS], F32)
-        normalized = [keep.tile([P, BS], F32, name="normalized%d" % ib) for ib in range(BLOCKS)]
-        halves = (slice(0, BS // 2), slice(BS // 2, BS))
-        inv_rows = {}
 
-        def normalise(ib, half):
-            cols = halves[half]
-            nc.vector.scalar_tensor_tensor(
-                out=normalized[ib][:, cols],
-                in0=adj[ib][:, cols],
-                scalar=inv_sqrt_deg[:, ib : ib + 1],
-                in1=inv_rows[half][:],
-                op0=ALU.mult,
-                op1=ALU.mult,
-            )
-            nc.sync.dma_start(out=out_0[ib * P : (ib + 1) * P, cols], in_=normalized[ib][:, cols])
+        def adjacency(ib):
+            one = slice(ib, ib + 1)
+            nc.scalar.activation(out=adj[:, ib, :], in_=dist[:, ib, :], func=ACT.Exp, scale=-1.0, accum_out=deg[:, one])
+            nc.sync.dma_start(out=out_1[ib * P : (ib + 1) * P, :], in_=adj[:, ib, :])
+            nc.gpsimd.tensor_tensor(out=inv_sqrt_deg[:, one], in0=deg[:, one], in1=minus_half[:, one], op=ALU.pow)
 
-        for half in (1, 0):
-            inv_rows[half] = flip_pool.tile([P, BS // 2], F32, name="inv_rows", tag="flip")
-            for side in (1, 0):
-                ib = 2 * half + side
-                one = slice(ib, ib + 1)
-                nc.scalar.activation(out=adj[ib][:], in_=dist[:, ib, :], func=ACT.Exp, scale=-1.0, accum_out=deg[:, one])
-                nc.sync.dma_start(out=out_1[ib * P : (ib + 1) * P, :], in_=adj[ib][:])
-                nc.gpsimd.tensor_tensor(out=inv_sqrt_deg[:, one], in0=deg[:, one], in1=minus_half[:, one], op=ALU.pow)
+        def inv_row(blocks):
+            bank = flip_pool.tile([P, len(blocks) * P], F32, name="inv_row", tag="flip")
+            for k, ib in enumerate(blocks):
                 nc.tensor.transpose(
-                    inv_rows[half][:, side * P : (side + 1) * P], inv_sqrt_deg[:, one].to_broadcast([P, P]), ident[:]
+                    bank[:, k * P : (k + 1) * P], inv_sqrt_deg[:, ib : ib + 1].to_broadcast([P, P]), ident[:]
                 )
-        for ib, half in ((3, 1), (2, 1), (3, 0), (2, 0), (1, 1), (1, 0), (0, 1), (0, 0)):
-            normalise(ib, half)
+            return bank
+
+        def scale_rows(ib, width):
+            nc.vector.tensor_scalar(
+                out=scaled[:, ib, 0:width], in0=adj[:, ib, 0:width], scalar1=inv_sqrt_deg[:, ib : ib + 1], scalar2=0.0,
+                op0=ALU.mult, op1=ALU.add,
+            )
+
+        def both(ib, lo, hi, inv):
+            nc.vector.scalar_tensor_tensor(
+                out=normalized[:, ib, lo:hi], in0=adj[:, ib, lo:hi], scalar=inv_sqrt_deg[:, ib : ib + 1], in1=inv,
+                op0=ALU.mult, op1=ALU.mult,
+            )
+
+        def scale_columns(first, jb, inv):
+            n = BLOCKS - first
+            cols = slice(jb * P, (jb + 1) * P)
+            nc.vector.tensor_tensor(
+                out=normalized[:, first:, cols], in0=scaled[:, first:, cols],
+                in1=inv.unsqueeze(1).to_broadcast([P, n, P]), op=ALU.mult,
+            )
+
+        def by_symmetry(bank, jb, blocks):
+            for ib in blocks:
+                nc.tensor.transpose(bank[:, ib, :], scaled[:, ib, jb * P : (jb + 1) * P], ident[:])
+
+        def finish_rows(jb, bank):
+            nc.scalar.activation(
+                out=normalized[:, jb, (jb + 1) * P :], in_=bank[:, jb + 1 :, :].rearrange("p b i -> p (b i)"),
+                func=ACT.Copy, scale=inv_sqrt_deg[:, jb : jb + 1],
+            )
+
+        def store(first, last, lo, hi):
+            nc.sync.dma_start(
+                out=out_0[first * P : (last + 1) * P, lo:hi].rearrange("(b p) j -> p b j", p=P),
+                in_=normalized[:, first : last + 1, lo:hi],
+            )
+
+        adjacency(3)
+        adjacency(2)
+        adjacency(1)
+        adjacency(0)
+        turned_1 = acc_pool.tile([P, BLOCKS, P], F32, name="turned_1", tag="acc")
+        turned_0 = acc_pool.tile([P, BLOCKS, P], F32, name="turned_0", tag="acc")
+        scale_rows(3, 2 * P)
+        right = inv_row([2, 3])
+        scale_rows(2, 2 * P)
+        by_symmetry(turned_1, 1, (2, 3))
+        both(2, 2 * P, BS, right[:])
+        left_1 = inv_row([1])
+        by_symmetry(turned_0, 0, (2, 3))
+        scale_rows(1, P)
+        both(3, 2 * P, BS, right[:])
+        store(2, 3, 2 * P, BS)
+        finish_rows(1, turned_1)
+        store(1, 1, 2 * P, BS)
+        left_0 = inv_row([0])
+        by_symmetry(turned_0, 0, (1,))
+        scale_columns(2, 1, left_1[:])
+        both(1, P, 2 * P, left_1[:])
+        finish_rows(0, turned_0)
+        store(0, 0, P, BS)
+        scale_columns(1, 0, left_0[:])
+        store(1, 3, 0, 2 * P)
+        both(0, 0, P, left_0[:])
+        store(0, 0, 0, P)

@@ -36,6 +36,8 @@ def tile_metric_learning_based_adjacency_matrix_kernel(tc, features, P_words, P_
         flip_pool = ctx.enter_context(tc.psum_pool(name="flip", bufs=4))
         ctx.enter_context(tc.manual_schedule())
 
+        zeros = keep.tile([P, BS], BF16)
+        nc.vector.memset(zeros[:].bitcast(I32), 0)
         p_planes = [keep.tile([P, D_PASSES, K_PASS], U8, name="pp%d" % c, align_bytes=64) for c in range(CHUNKS)]
         for c in range(CHUNKS):
             nc.vector.memset(p_planes[c][:].rearrange("p g n -> p (g n)").bitcast(I32), 0)
@@ -50,8 +52,6 @@ def tile_metric_learning_based_adjacency_matrix_kernel(tc, features, P_words, P_
         warm = keep.tile([P, 1], F32)
         nc.scalar.activation(out=warm[:], in_=sqrt_floor[:], func=ACT.Sqrt)
 
-        zeros = keep.tile([P, BS], BF16)
-        nc.gpsimd.memset(zeros[:], 0.0)
 
         def warm_up(matmuls):
             idle = acc_pool.tile([P, BS], F32, name="idle", tag="acc")
@@ -159,6 +159,9 @@ def tile_metric_learning_based_adjacency_matrix_kernel(tc, features, P_words, P_
                 out=z_rows[ib][:, c * K_PASS : (c + 1) * K_PASS].rearrange("i (u p e) -> i u p e", u=2, e=2),
                 in_=zt[:].rearrange("i (p u e) -> i u p e", u=2, e=2),
             )
+            return ib, c, zt
+
+        def square(ib, c, zt):
             if ib in VECTOR_NORMS:
                 nc.vector.bn_stats(out=stats[ib][:, c, :], in_=zt[:])
             else:
@@ -183,12 +186,12 @@ def tile_metric_learning_based_adjacency_matrix_kernel(tc, features, P_words, P_
             for ib in blocks:
                 own = slice(ib * P, (ib + 1) * P)
                 nc.tensor.transpose(spread[:, own], n_col[:, ib : ib + 1].to_broadcast([P, P]), ident[:])
-            for ib in blocks:
-                own = slice(ib * P, (ib + 1) * P)
-                nc.vector.tensor_add(out=n_diag[:, own], in0=spread[:, own], in1=off_scale[:])
             some = slice(blocks[0] * P, (blocks[-1] + 1) * P)
             if blocks[-1] < BLOCKS - 1:
                 copy(out=n_rows[:, some], in_=spread[:, some])
+            for ib in blocks:
+                own = slice(ib * P, (ib + 1) * P)
+                nc.vector.tensor_add(out=n_diag[:, own], in0=spread[:, own], in1=off_scale[:])
 
         dist = keep.tile([P, BLOCKS, BS], F32)
         gram_of = {}
@@ -251,64 +254,63 @@ def tile_metric_learning_based_adjacency_matrix_kernel(tc, features, P_words, P_
         warm_up(2)
         unload(f0, scalar=(1,))
         quantise(f0)
-        project(0, 0)
+        square(*project(0, 0))
         f1 = flip_features(1)
         unload(f1)
         quantise(f1)
-        project(0, 1)
-        project(1, 0)
-        project(1, 1)
-        project(0, 2)
-        project(0, 3)
+        square(*project(0, 1))
+        square(*project(1, 0))
+        square(*project(1, 1))
+        square(*project(0, 2))
+        square(*project(0, 3))
         f2 = flip_features(2) + flip_z(0, (0, 1)) + flip_z(1, (0, 1))
         unload(f2)
         quantise(f2)
-        project(1, 2)
-        project(1, 3)
-        project(2, 0)
-        project(2, 1)
+        square(*project(1, 2))
+        square(*project(1, 3))
+        square(*project(2, 0))
+        square(*project(2, 1))
         norm_columns([0, 1])
         f3 = flip_features(3) + flip_z(0, (2, 3)) + flip_z(1, (2, 3))
         unload(f3)
         norm_rows([0, 1], nc.vector.tensor_copy)
         quantise(f3)
-        project(2, 2)
-        project(2, 3)
-        project(3, 0)
+        square(*project(2, 2))
+        square(*project(2, 3))
+        square(*project(3, 0))
         gram(0, every)
         gram(1, every)
         distances([(0, 0, 128), (1, 0, 256)])
-        project(3, 1)
+        square(*project(3, 1))
         norm_columns([2])
-        z2 = flip_z(2, (0, 1)) + flip_z(2, (2, 3))
+        z2 = flip_z(2, (0, 1)) + flip_z(2, (2, 3)) + flip_z(3, (0,))
         unload(z2)
         quantise(z2)
         norm_rows([2], nc.scalar.copy)
-        project(3, 2)
-        z3 = flip_z(3, (0, 1))
-        unload(z3)
-        quantise(z3)
-        project(3, 3)
-        z3 = flip_z(3, (2,))
+        z32 = project(3, 2)
+        z33 = project(3, 3)
+        square(*z32)
+        square(*z33)
+        z31 = flip_z(3, (1,))
+        z32 = flip_z(3, (2,))
+        unload(z31)
         gram(2, every, 0, 256)
-        unload(z3)
+        unload(z32)
+        quantise(z31 + z32)
+        z33 = flip_z(3, (3,))
+        unload(z33)
         near = squared(2, 0, 256)
-        quantise(z3)
-        z3 = flip_z(3, (3,))
-        rooted(*near)
-        unload(z3)
-        norm_columns([3])
-        quantise(z3)
         gram(2, every, 256, 384)
-        gram(3, (0, 1, 2))
+        quantise(z33)
+        norm_columns([3])
+        rooted(*near)
+        gram(3, every)
         own_2 = squared(2, 256, 384)
-        norm_rows([3], None)
-        gram(3, (3,))
-        others_3 = squared(3, 0, 384)
         rooted(*own_2)
-        own_3 = squared(3, 384, 512)
+        others_3 = squared(3, 0, 384)
+        norm_rows([3], None)
         rooted(*others_3)
-        rooted(*own_3)
+        distances([(3, 384, 512)])
         mirror(1)
         mirror(2)
         mirror(3, 0, 2)
@@ -326,13 +328,8 @@ def tile_metric_learning_based_adjacency_matrix_kernel(tc, features, P_words, P_
             nc.sync.dma_start(out=out_1[ib * P : (ib + 1) * P, :], in_=adj[:, ib, :])
             nc.gpsimd.tensor_tensor(out=inv_sqrt_deg[:, one], in0=deg[:, one], in1=minus_half[:, one], op=ALU.pow)
 
-        def inv_row(blocks):
-            bank = flip_pool.tile([P, len(blocks) * P], F32, name="inv_row", tag="flip")
-            for k, ib in enumerate(blocks):
-                nc.tensor.transpose(
-                    bank[:, k * P : (k + 1) * P], inv_sqrt_deg[:, ib : ib + 1].to_broadcast([P, P]), ident[:]
-                )
-            return bank
+        def inv_row(bank, k, ib):
+            nc.tensor.transpose(bank[:, k * P : (k + 1) * P], inv_sqrt_deg[:, ib : ib + 1].to_broadcast([P, P]), ident[:])
 
         def scale_rows(ib, width):
             nc.vector.tensor_scalar(
@@ -376,25 +373,33 @@ def tile_metric_learning_based_adjacency_matrix_kernel(tc, features, P_words, P_
         adjacency(0)
         turned_1 = acc_pool.tile([P, BLOCKS, P], F32, name="turned_1", tag="acc")
         turned_0 = acc_pool.tile([P, BLOCKS, P], F32, name="turned_0", tag="acc")
+        right = flip_pool.tile([P, 2 * P], F32, name="right", tag="flip")
+        left_1 = flip_pool.tile([P, P], F32, name="left_1", tag="flip")
+        left_0 = flip_pool.tile([P, P], F32, name="left_0", tag="flip")
+        inv_row(right, 1, 3)
         scale_rows(3, 2 * P)
-        right = inv_row([2, 3])
+        by_symmetry(turned_1, 1, (3,))
+        by_symmetry(turned_0, 0, (3,))
+        inv_row(right, 0, 2)
         scale_rows(2, 2 * P)
-        by_symmetry(turned_1, 1, (2, 3))
+        by_symmetry(turned_1, 1, (2,))
+        by_symmetry(turned_0, 0, (2,))
         both(2, 2 * P, BS, right[:])
-        left_1 = inv_row([1])
-        by_symmetry(turned_0, 0, (2, 3))
+        store(2, 2, 2 * P, BS)
+        inv_row(left_1, 0, 1)
         scale_rows(1, P)
+        by_symmetry(turned_0, 0, (1,))
         both(3, 2 * P, BS, right[:])
-        store(2, 3, 2 * P, BS)
+        store(3, 3, 2 * P, BS)
         finish_rows(1, turned_1)
         store(1, 1, 2 * P, BS)
-        left_0 = inv_row([0])
-        by_symmetry(turned_0, 0, (1,))
         scale_columns(2, 1, left_1[:])
         both(1, P, 2 * P, left_1[:])
+        store(1, 3, P, 2 * P)
+        inv_row(left_0, 0, 0)
         finish_rows(0, turned_0)
         store(0, 0, P, BS)
         scale_columns(1, 0, left_0[:])
-        store(1, 3, 0, 2 * P)
+        store(1, 3, 0, P)
         both(0, 0, P, left_0[:])
         store(0, 0, 0, P)

@@ -69,15 +69,15 @@ def tile_metric_learning_based_adjacency_matrix_kernel(tc, features, P_words, P_
                 nc.sync.dma_start(out=x_sb[ib][:, cols], in_=features[ib * P : (ib + 1) * P, cols])
 
         def load_p(c):
+            nc.sync.dma_start(
+                out=p_words[c][:].bitcast(I32),
+                in_=words_i32[:, :, c * (K_PASS // 2) : (c + 1) * (K_PASS // 2)].rearrange("g p w -> p g w"),
+            )
             for q in range(4):
                 nc.sync.dma_start(
                     out=p_planes[c][q : P : 32, :, :].bitcast(I32),
                     in_=scales_i32[:, q : 16 : 4, c * (K_PASS // 4) : (c + 1) * (K_PASS // 4)].rearrange("g q n -> q g n"),
                 )
-            nc.sync.dma_start(
-                out=p_words[c][:].bitcast(I32),
-                in_=words_i32[:, :, c * (K_PASS // 2) : (c + 1) * (K_PASS // 2)].rearrange("g p w -> p g w"),
-            )
 
         load_features(0, 2)
         load_p(0)
@@ -100,20 +100,20 @@ def tile_metric_learning_based_adjacency_matrix_kernel(tc, features, P_words, P_
         n_rows = keep.tile([P, BS], F32)
         n_diag = keep.tile([P, BS], F32)
 
-        def flip_features(ib):
+        def flip_features(ib, passes):
             words = x_sb[ib][:].bitcast(F32)
             jobs = []
-            for h in range(2):
+            for g in range(0, D_PASSES, passes):
                 bank = flip_pool.tile([P, 2, 2, P], F32, name="xbank", tag="flip")
-                for a in range(2):
-                    g = 2 * h + a
+                for a in range(passes):
                     for u in range(2):
-                        nc.tensor.transpose(bank[:, a, u, :], words[:, 256 * g + u : 256 * (g + 1) : 2], ident[:])
-                half = slice(2 * h, 2 * h + 2)
-                codes = f_codes[ib][:, half].rearrange("p g i -> p (g i)")
-                scales = f_scales[ib][:, half].rearrange("p g i -> p (g i)")
-                grouped = f_grouped[ib][:, half]
-                jobs.append((bank[:], grouped, [(codes, scales, grouped.rearrange("p g i t -> p (g i t)"))]))
+                        pairs = words[:, 256 * (g + a) + u : 256 * (g + a + 1) : 2]
+                        nc.tensor.transpose(bank[:, a, u, :], pairs, ident[:])
+                some = slice(g, g + passes)
+                codes = f_codes[ib][:, some].rearrange("p g i -> p (g i)")
+                scales = f_scales[ib][:, some].rearrange("p g i -> p (g i)")
+                grouped = f_grouped[ib][:, some]
+                jobs.append((bank[:, 0:passes], grouped, [(codes, scales, grouped.rearrange("p g i t -> p (g i t)"))]))
             return jobs
 
         def flip_z(ib, chunks):
@@ -198,12 +198,15 @@ def tile_metric_learning_based_adjacency_matrix_kernel(tc, features, P_words, P_
 
         def gram(ib, chunks, lo=0, hi=None):
             hi = (ib + 1) * P if hi is None else hi
-            if ib not in gram_of:
-                gram_of[ib] = acc_pool.tile([P, BS], F32, name="gram", tag="acc")
+            if (ib, lo) not in gram_of:
+                if lo == 0:
+                    gram_of[ib, lo] = acc_pool.tile([P, BS], F32, name="gram", tag="acc")
+                else:
+                    gram_of[ib, lo] = flip_pool.tile([P, BS], F32, name="gram_part", tag="flip")
             rows = slice(ib * P, (ib + 1) * P)
             for c in chunks:
                 nc.tensor.matmul_mx(
-                    out=gram_of[ib][:, lo:hi],
+                    out=gram_of[ib, lo][:, lo:hi],
                     lhsT=z_codes[c][:, rows].bitcast(FP8X4),
                     lhsT_scale=z_scales[c][:, rows],
                     rhs=z_codes[c][:, lo:hi].bitcast(FP8X4),
@@ -214,11 +217,12 @@ def tile_metric_learning_based_adjacency_matrix_kernel(tc, features, P_words, P_
 
         def squared(ib, lo, hi):
             own = ib * P
+            bank = gram_of.get((ib, lo), gram_of[ib, 0])
             sq = work.tile([P, BS], F32, name="sq", tag="sq", bufs=4)
             for a, b, row in ((lo, min(hi, own), n_rows), (max(lo, own), hi, n_diag)):
                 if a < b:
                     nc.vector.scalar_tensor_tensor(
-                        out=sq[:, a:b], in0=gram_of[ib][:, a:b], scalar=-2.0, in1=row[:, a:b], op0=ALU.mult, op1=ALU.add
+                        out=sq[:, a:b], in0=bank[:, a:b], scalar=-2.0, in1=row[:, a:b], op0=ALU.mult, op1=ALU.add
                     )
             return ib, lo, hi, sq
 
@@ -250,12 +254,12 @@ def tile_metric_learning_based_adjacency_matrix_kernel(tc, features, P_words, P_
 
         every = range(CHUNKS)
         warm_up(3)
-        f0 = flip_features(0)
+        f0 = flip_features(0, 1)
         warm_up(2)
-        unload(f0, scalar=(1,))
+        unload(f0, scalar=(1, 3))
         quantise(f0)
         square(*project(0, 0))
-        f1 = flip_features(1)
+        f1 = flip_features(1, 2)
         unload(f1)
         quantise(f1)
         square(*project(0, 1))
@@ -263,7 +267,7 @@ def tile_metric_learning_based_adjacency_matrix_kernel(tc, features, P_words, P_
         square(*project(1, 1))
         square(*project(0, 2))
         square(*project(0, 3))
-        f2 = flip_features(2) + flip_z(0, (0, 1)) + flip_z(1, (0, 1))
+        f2 = flip_features(2, 2) + flip_z(0, (0, 1)) + flip_z(1, (0, 1))
         unload(f2)
         quantise(f2)
         square(*project(1, 2))
@@ -271,7 +275,7 @@ def tile_metric_learning_based_adjacency_matrix_kernel(tc, features, P_words, P_
         square(*project(2, 0))
         square(*project(2, 1))
         norm_columns([0, 1])
-        f3 = flip_features(3) + flip_z(0, (2, 3)) + flip_z(1, (2, 3))
+        f3 = flip_features(3, 2) + flip_z(0, (2, 3)) + flip_z(1, (2, 3))
         unload(f3)
         norm_rows([0, 1], nc.vector.tensor_copy)
         quantise(f3)
@@ -299,12 +303,13 @@ def tile_metric_learning_based_adjacency_matrix_kernel(tc, features, P_words, P_
         quantise(z31 + z32)
         z33 = flip_z(3, (3,))
         unload(z33)
-        near = squared(2, 0, 256)
+        gram(3, (0,))
         gram(2, every, 256, 384)
         quantise(z33)
+        near = squared(2, 0, 256)
         norm_columns([3])
         rooted(*near)
-        gram(3, every)
+        gram(3, (1, 2, 3))
         own_2 = squared(2, 256, 384)
         rooted(*own_2)
         others_3 = squared(3, 0, 384)

@@ -100,14 +100,26 @@ def tile_metric_learning_based_adjacency_matrix_kernel(tc, features, P_words, P_
         n_rows = keep.tile([P, BS], F32)
         n_diag = keep.tile([P, BS], F32)
 
+        x_ordered = {}
+
+        def order_features(ib):
+            x_ordered[ib] = keep.tile([P, D], BF16, name="xo%d" % ib)
+            nc.vector.tensor_copy(
+                out=x_ordered[ib][:].bitcast(F32).rearrange("i (g u p) -> i g u p", u=2, p=P),
+                in_=x_sb[ib][:].bitcast(F32).rearrange("i (g p u) -> i g u p", u=2, p=P),
+            )
+
         def flip_features(ib, passes):
-            words = x_sb[ib][:].bitcast(F32)
+            words = (x_ordered[ib] if ib in x_ordered else x_sb[ib])[:].bitcast(F32)
             jobs = []
             for g in range(0, D_PASSES, passes):
                 bank = flip_pool.tile([P, 2, 2, P], F32, name="xbank", tag="flip")
                 for a in range(passes):
                     for u in range(2):
-                        pairs = words[:, 256 * (g + a) + u : 256 * (g + a + 1) : 2]
+                        if ib in x_ordered:
+                            pairs = words[:, 256 * (g + a) + P * u : 256 * (g + a) + P * (u + 1)]
+                        else:
+                            pairs = words[:, 256 * (g + a) + u : 256 * (g + a + 1) : 2]
                         nc.tensor.transpose(bank[:, a, u, :], pairs, ident[:])
                 some = slice(g, g + passes)
                 codes = f_codes[ib][:, some].rearrange("p g i -> p (g i)")
@@ -253,7 +265,7 @@ def tile_metric_learning_based_adjacency_matrix_kernel(tc, features, P_words, P_
             nc.vector.tensor_copy(out=dist[:, lo:hi, own], in_=mirrored[:, lo:hi, :])
 
         every = range(CHUNKS)
-        warm_up(3)
+        warm_up(6)
         f0 = flip_features(0, 1)
         warm_up(2)
         unload(f0, scalar=(1, 3))
@@ -265,20 +277,30 @@ def tile_metric_learning_based_adjacency_matrix_kernel(tc, features, P_words, P_
         square(*project(0, 1))
         square(*project(1, 0))
         square(*project(1, 1))
+        order_features(2)
         square(*project(0, 2))
         square(*project(0, 3))
-        f2 = flip_features(2, 2) + flip_z(0, (0, 1)) + flip_z(1, (0, 1))
-        unload(f2)
-        quantise(f2)
+        order_features(3)
+        x2 = flip_features(2, 2)
+        za = flip_z(0, (0, 1)) + flip_z(1, (0, 1))
+        unload(x2)
+        unload(za[:1])
+        quantise(x2)
+        unload(za[1:])
+        quantise(za)
         square(*project(1, 2))
         square(*project(1, 3))
         square(*project(2, 0))
         square(*project(2, 1))
         norm_columns([0, 1])
-        f3 = flip_features(3, 2) + flip_z(0, (2, 3)) + flip_z(1, (2, 3))
-        unload(f3)
+        x3 = flip_features(3, 2)
+        zb = flip_z(0, (2, 3)) + flip_z(1, (2, 3))
+        unload(x3)
+        unload(zb[:1])
+        quantise(x3)
+        unload(zb[1:])
         norm_rows([0, 1], nc.vector.tensor_copy)
-        quantise(f3)
+        quantise(zb)
         square(*project(2, 2))
         square(*project(2, 3))
         square(*project(3, 0))

@@ -265,7 +265,7 @@ def tile_metric_learning_based_adjacency_matrix_kernel(tc, features, P_words, P_
             nc.vector.tensor_copy(out=dist[:, lo:hi, own], in_=mirrored[:, lo:hi, :])
 
         every = range(CHUNKS)
-        warm_up(6)
+        warm_up(5)
         f0 = flip_features(0, 1)
         warm_up(2)
         unload(f0, scalar=(1, 3))
@@ -286,7 +286,7 @@ def tile_metric_learning_based_adjacency_matrix_kernel(tc, features, P_words, P_
         unload(x2)
         unload(za[:1])
         quantise(x2)
-        unload(za[1:])
+        unload(za[1:], scalar=(0,))
         quantise(za)
         square(*project(1, 2))
         square(*project(1, 3))
@@ -298,7 +298,7 @@ def tile_metric_learning_based_adjacency_matrix_kernel(tc, features, P_words, P_
         unload(x3)
         unload(zb[:1])
         quantise(x3)
-        unload(zb[1:])
+        unload(zb[1:], scalar=(0,))
         norm_rows([0, 1], nc.vector.tensor_copy)
         quantise(zb)
         square(*project(2, 2))
@@ -342,6 +342,7 @@ def tile_metric_learning_based_adjacency_matrix_kernel(tc, features, P_words, P_
         mirror(2)
         mirror(3, 0, 2)
         mirror(3, 2, 3)
+        warm_up(4)
 
         adj = keep.tile([P, BLOCKS, BS], F32)
         normalized = keep.tile([P, BLOCKS, BS], F32)

@@ -38,9 +38,11 @@ def tile_metric_learning_based_adjacency_matrix_kernel(tc, features, P_words, P_
 
         zeros = keep.tile([P, BS], BF16)
         nc.vector.memset(zeros[:].bitcast(I32), 0)
-        p_planes = [keep.tile([P, D_PASSES, K_PASS], U8, name="pp%d" % c, align_bytes=64) for c in range(CHUNKS)]
-        for c in range(CHUNKS):
-            nc.vector.memset(p_planes[c][:].rearrange("p g n -> p (g n)").bitcast(I32), 0)
+        p_planes = [
+            keep.tile([P, D_PASSES, n * K_PASS], U8, name="pp%d" % k, align_bytes=64) for k, n in enumerate((1, 1, 2))
+        ]
+        for plane in p_planes:
+            nc.vector.memset(plane[:].rearrange("p g n -> p (g n)").bitcast(I32), 0)
         sqrt_floor = keep.tile([P, 1], F32)
         nc.vector.memset(sqrt_floor[:], SQRT_FLOOR)
         minus_half = keep.tile([P, BLOCKS], F32)
@@ -73,17 +75,22 @@ def tile_metric_learning_based_adjacency_matrix_kernel(tc, features, P_words, P_
                 out=p_words[c][:].bitcast(I32),
                 in_=words_i32[:, :, c * (K_PASS // 2) : (c + 1) * (K_PASS // 2)].rearrange("g p w -> p g w"),
             )
+
+        def load_scales(k, c, n):
             for q in range(4):
                 nc.sync.dma_start(
-                    out=p_planes[c][q : P : 32, :, :].bitcast(I32),
-                    in_=scales_i32[:, q : 16 : 4, c * (K_PASS // 4) : (c + 1) * (K_PASS // 4)].rearrange("g q n -> q g n"),
+                    out=p_planes[k][q : P : 32, :, :].bitcast(I32),
+                    in_=scales_i32[:, q : 16 : 4, c * (K_PASS // 4) : (c + n) * (K_PASS // 4)].rearrange("g q n -> q g n"),
                 )
 
         load_features(0, 2)
         load_p(0)
+        load_scales(0, 0, 1)
         load_features(1, 1)
         load_p(1)
+        load_scales(1, 1, 1)
         load_p(2)
+        load_scales(2, 2, 2)
         load_p(3)
         load_features(2, 1)
         load_features(3, 1)
@@ -163,7 +170,7 @@ def tile_metric_learning_based_adjacency_matrix_kernel(tc, features, P_words, P_
                     lhsT=f_codes[ib][:, g, :].bitcast(FP8X4),
                     lhsT_scale=f_scales[ib][:, g, :],
                     rhs=p_words[c][:, g, :].bitcast(FP4X4),
-                    rhs_scale=p_planes[c][:, g, :],
+                    rhs_scale=p_planes[min(c, 2)][:, g, max(c - 2, 0) * K_PASS : (max(c - 2, 0) + 1) * K_PASS],
                     start=(g == 0),
                     stop=(g == D_PASSES - 1),
                 )
@@ -272,6 +279,7 @@ def tile_metric_learning_based_adjacency_matrix_kernel(tc, features, P_words, P_
         quantise(f0)
         square(*project(0, 0))
         f1 = flip_features(1, 2)
+        warm_up(1)
         unload(f1)
         quantise(f1)
         square(*project(0, 1))
@@ -342,7 +350,7 @@ def tile_metric_learning_based_adjacency_matrix_kernel(tc, features, P_words, P_
         mirror(2)
         mirror(3, 0, 2)
         mirror(3, 2, 3)
-        warm_up(4)
+        warm_up(6)
 
         adj = keep.tile([P, BLOCKS, BS], F32)
         normalized = keep.tile([P, BLOCKS, BS], F32)

@@ -20,7 +20,6 @@ K_PASS = P * PACK
 BS, D, R = 512, 2048, 2048
 BLOCKS = BS // P
 D_PASSES = D // K_PASS
-VECTOR_NORMS = (1,)
 CHUNKS = R // K_PASS
 SQRT_FLOOR = 2.0 ** -116
 
@@ -102,7 +101,6 @@ def tile_metric_learning_based_adjacency_matrix_kernel(tc, features, P_words, P_
         z_codes = [keep.tile([P, BS], U32, name="zc%d" % c, align_bytes=64) for c in range(CHUNKS)]
         z_scales = [keep.tile([P, BS], U8, name="zs%d" % c, align_bytes=64) for c in range(CHUNKS)]
         n_parts = keep.tile([P, BLOCKS, CHUNKS], F32)
-        stats = {ib: keep.tile([P, CHUNKS, 6], F32, name="st%d" % ib) for ib in VECTOR_NORMS}
         n_col = keep.tile([P, BLOCKS], F32)
         n_rows = keep.tile([P, BS], F32)
         n_diag = keep.tile([P, BS], F32)
@@ -181,24 +179,12 @@ def tile_metric_learning_based_adjacency_matrix_kernel(tc, features, P_words, P_
             return ib, c, zt
 
         def square(ib, c, zt):
-            if ib in VECTOR_NORMS:
-                nc.vector.bn_stats(out=stats[ib][:, c, :], in_=zt[:])
-            else:
-                squares = work.tile([P, BS], F32, name="squares", tag="squares")
-                nc.scalar.activation(out=squares[:], in_=zt[:], func=ACT.Square, accum_out=n_parts[:, ib, c : c + 1])
+            squares = work.tile([P, BS], F32, name="squares", tag="squares")
+            nc.scalar.activation(out=squares[:], in_=zt[:], func=ACT.Square, accum_out=n_parts[:, ib, c : c + 1])
 
         def norm_columns(blocks):
-            for ib in blocks:
-                one = n_col[:, ib : ib + 1]
-                if ib in VECTOR_NORMS:
-                    moments = work.tile([P, 2], F32, name="moments", tag="moments")
-                    nc.vector.bn_aggr(out=moments[:], in_=stats[ib][:].rearrange("p c s -> p (c s)"))
-                    nc.vector.scalar_tensor_tensor(
-                        out=one, in0=moments[:, 0:1], scalar=moments[:, 0:1], in1=moments[:, 1:2], op0=ALU.mult, op1=ALU.add
-                    )
-                    nc.vector.tensor_scalar(out=one, in0=one, scalar1=float(R), scalar2=0.0, op0=ALU.mult, op1=ALU.add)
-                else:
-                    nc.vector.tensor_reduce(out=one, in_=n_parts[:, ib, :], op=ALU.add, axis=AX.X)
+            some = slice(blocks[0], blocks[-1] + 1)
+            nc.vector.tensor_reduce(out=n_col[:, some], in_=n_parts[:, some, :], op=ALU.add, axis=AX.X)
 
         def norm_rows(blocks, copy):
             spread = acc_pool.tile([P, BS], F32, name="spread", tag="acc")

@@ -90,8 +90,8 @@ def tile_metric_learning_based_adjacency_matrix_kernel(tc, features, P_words, P_
         load_scales(1, 1, 1)
         load_p(2)
         load_scales(2, 2, 2)
-        load_p(3)
         load_features(2, 1)
+        load_p(3)
         load_features(3, 1)
 
         f_grouped = [keep.tile([P, D_PASSES, P, PACK], BF16, name="fg%d" % ib, align_bytes=64) for ib in range(BLOCKS)]
@@ -271,10 +271,9 @@ def tile_metric_learning_based_adjacency_matrix_kernel(tc, features, P_words, P_
         square(*project(0, 1))
         square(*project(1, 0))
         square(*project(1, 1))
-        order_features(2)
         square(*project(0, 2))
-        square(*project(0, 3))
-        order_features(3)
+        order_features(2)
+        square(*project(1, 2))
         x2 = flip_features(2, 2)
         za = flip_z(0, (0, 1)) + flip_z(1, (0, 1))
         unload(x2)
@@ -282,8 +281,9 @@ def tile_metric_learning_based_adjacency_matrix_kernel(tc, features, P_words, P_
         quantise(x2)
         unload(za[1:], scalar=(0,))
         quantise(za)
-        square(*project(1, 2))
+        square(*project(0, 3))
         square(*project(1, 3))
+        order_features(3)
         square(*project(2, 0))
         square(*project(2, 1))
         norm_columns([0, 1])

from contextlib import ExitStack

import concourse.mybir as mybir
from concourse.masks import make_identity

F32 = mybir.dt.float32
BF16 = mybir.dt.bfloat16
I32 = mybir.dt.int32
U32 = mybir.dt.uint32
U8 = mybir.dt.uint8
FP8X4 = mybir.dt.float8_e4m3fn_x4
FP4X4 = mybir.dt.float4_e2m1fn_x4
ACT = mybir.ActivationFunctionType
ALU = mybir.AluOpType
AX = mybir.AxisListType

P = 128
PACK = 4
K_PASS = P * PACK
BS, D, R = 512, 2048, 2048
BLOCKS = BS // P
D_PASSES = D // K_PASS
CHUNKS = R // K_PASS
SQRT_FLOOR = 2.0 ** -116

FLOPS = 2 * BS * D * R + 2 * BS * BS * R


def tile_metric_learning_based_adjacency_matrix_kernel(tc, features, P_words, P_scales, out_0, out_1):
    nc = tc.nc
    with ExitStack() as ctx:
        keep = ctx.enter_context(tc.tile_pool(name="keep", bufs=1))
        work = ctx.enter_context(tc.tile_pool(name="work", bufs=2))
        acc_pool = ctx.enter_context(tc.psum_pool(name="acc", bufs=4))
        flip_pool = ctx.enter_context(tc.psum_pool(name="flip", bufs=4))
        ctx.enter_context(tc.manual_schedule())

        zeros = keep.tile([P, BS], BF16)
        nc.vector.memset(zeros[:].bitcast(I32), 0)
        p_planes = [
            keep.tile([P, D_PASSES, n * K_PASS], U8, name="pp%d" % k, align_bytes=64) for k, n in enumerate((1, 1, 2))
        ]
        for plane in p_planes:
            nc.vector.memset(plane[:].rearrange("p g n -> p (g n)").bitcast(I32), 0)
        sqrt_floor = keep.tile([P, 1], F32)
        nc.vector.memset(sqrt_floor[:], SQRT_FLOOR)
        minus_half = keep.tile([P, BLOCKS], F32)
        nc.vector.memset(minus_half[:], -0.5)
        ident = keep.tile([P, P], F32)
        make_identity(nc, ident[:])
        off_scale = keep.tile([P, P], F32)
        nc.vector.tensor_scalar(out=off_scale[:], in0=ident[:], scalar1=-3.0e38, scalar2=0.0, op0=ALU.mult, op1=ALU.add)
        warm = keep.tile([P, 1], F32)
        nc.scalar.activation(out=warm[:], in_=sqrt_floor[:], func=ACT.Sqrt)


        def warm_up(matmuls):
            idle = acc_pool.tile([P, BS], F32, name="idle", tag="acc")
            for k in range(matmuls):
                nc.tensor.matmul(out=idle[:], lhsT=zeros[:, 0:P], rhs=zeros[:], start=True, stop=True)

        x_sb = [keep.tile([P, D], BF16, name="x%d" % ib) for ib in range(BLOCKS)]
        p_words = [keep.tile([P, D_PASSES, 2 * K_PASS], U8, name="pw%d" % c, align_bytes=64) for c in range(CHUNKS)]
        scales_i32 = P_scales.bitcast(I32)
        words_i32 = P_words.bitcast(I32)

        def load_features(ib, pieces):
            for s in range(pieces):
                cols = slice(s * D // pieces, (s + 1) * D // pieces)
                nc.sync.dma_start(out=x_sb[ib][:, cols], in_=features[ib * P : (ib + 1) * P, cols])

        def load_p(c):
            nc.sync.dma_start(
                out=p_words[c][:].bitcast(I32),
                in_=words_i32[:, :, c * (K_PASS // 2) : (c + 1) * (K_PASS // 2)].rearrange("g p w -> p g w"),
            )

        def load_scales(k, c, n):
            for q in range(4):
                nc.sync.dma_start(
                    out=p_planes[k][q : P : 32, :, :].bitcast(I32),
                    in_=scales_i32[:, q : 16 : 4, c * (K_PASS // 4) : (c + n) * (K_PASS // 4)].rearrange("g q n -> q g n"),
                )

        load_features(0, 2)
        load_p(0)
        load_scales(0, 0, 1)
        load_features(1, 1)
        load_p(1)
        load_scales(1, 1, 1)
        load_p(2)
        load_scales(2, 2, 2)
        load_features(2, 1)
        load_p(3)
        load_features(3, 1)

        f_grouped = [keep.tile([P, D_PASSES, P, PACK], BF16, name="fg%d" % ib, align_bytes=64) for ib in range(BLOCKS)]
        f_codes = [keep.tile([P, D_PASSES, P], U32, name="fc%d" % ib, align_bytes=64) for ib in range(BLOCKS)]
        f_scales = [keep.tile([P, D_PASSES, P], U8, name="fs%d" % ib, align_bytes=64) for ib in range(BLOCKS)]
        z_rows = [keep.tile([P, R], BF16, name="zr%d" % ib, align_bytes=64) for ib in range(BLOCKS)]
        z_codes = [keep.tile([P, BS], U32, name="zc%d" % c, align_bytes=64) for c in range(CHUNKS)]
        z_scales = [keep.tile([P, BS], U8, name="zs%d" % c, align_bytes=64) for c in range(CHUNKS)]
        n_parts = keep.tile([P, BLOCKS, CHUNKS], F32)
        n_col = keep.tile([P, BLOCKS], F32)
        n_rows = keep.tile([P, BS], F32)
        n_diag = keep.tile([P, BS], F32)

        x_ordered = {}

        def order_features(ib):
            x_ordered[ib] = keep.tile([P, D], BF16, name="xo%d" % ib)
            nc.vector.tensor_copy(
                out=x_ordered[ib][:].bitcast(F32).rearrange("i (g u p) -> i g u p", u=2, p=P),
                in_=x_sb[ib][:].bitcast(F32).rearrange("i (g p u) -> i g u p", u=2, p=P),
            )

        def flip_features(ib, passes):
            words = (x_ordered[ib] if ib in x_ordered else x_sb[ib])[:].bitcast(F32)
            jobs = []
            for g in range(0, D_PASSES, passes):
                bank = flip_pool.tile([P, 2, 2, P], F32, name="xbank", tag="flip")
                for a in range(passes):
                    for u in range(2):
                        if ib in x_ordered:
                            pairs = words[:, 256 * (g + a) + P * u : 256 * (g + a) + P * (u + 1)]
                        else:
                            pairs = words[:, 256 * (g + a) + u : 256 * (g + a + 1) : 2]
                        nc.tensor.transpose(bank[:, a, u, :], pairs, ident[:])
                some = slice(g, g + passes)
                codes = f_codes[ib][:, some].rearrange("p g i -> p (g i)")
                scales = f_scales[ib][:, some].rearrange("p g i -> p (g i)")
                grouped = f_grouped[ib][:, some]
                jobs.append((bank[:, 0:passes], grouped, [(codes, scales, grouped.rearrange("p g i t -> p (g i t)"))]))
            return jobs

        def flip_z(ib, chunks):
            words = z_rows[ib][:].bitcast(F32)
            bank = flip_pool.tile([P, 2, 2, P], F32, name="zbank", tag="flip")
            grouped = work.tile([P, 2, P, PACK], BF16, name="zg", tag="zg", bufs=4, align_bytes=64)
            rows = slice(ib * P, (ib + 1) * P)
            quants = []
            for a, c in enumerate(chunks):
                for u in range(2):
                    nc.tensor.transpose(bank[:, a, u, :], words[:, 256 * c + P * u : 256 * c + P * (u + 1)], ident[:])
                quants.append((z_codes[c][:, rows], z_scales[c][:, rows], grouped[:, a].rearrange("p i t -> p (i t)")))
            n = len(chunks)
            return [(bank[:, 0:n], grouped[:, 0:n], quants)]

        def unload(jobs, scalar=()):
            for k, (bank, grouped, quants) in enumerate(jobs):
                target = grouped.rearrange("p a i t -> p (a i t)").bitcast(F32).rearrange("p (a i u) -> p a i u", u=2, i=P)
                source = bank.rearrange("p a u i -> p a i u")
                if k in scalar:
                    nc.scalar.copy(out=target, in_=source)
                else:
                    nc.vector.tensor_copy(out=target, in_=source)

        def quantise(jobs):
            for bank, grouped, quants in jobs:
                for codes, scales, values in quants:
                    nc.vector.quantize_mx(out=codes.bitcast(FP8X4), scales=scales, in_=values)

        def project(ib, c):
            zt = acc_pool.tile([P, BS], F32, name="zt", tag="acc")
            for g in range(D_PASSES):
                nc.tensor.matmul_mx(
                    out=zt[:],
                    lhsT=f_codes[ib][:, g, :].bitcast(FP8X4),
                    lhsT_scale=f_scales[ib][:, g, :],
                    rhs=p_words[c][:, g, :].bitcast(FP4X4),
                    rhs_scale=p_planes[min(c, 2)][:, g, max(c - 2, 0) * K_PASS : (max(c - 2, 0) + 1) * K_PASS],
                    start=(g == 0),
                    stop=(g == D_PASSES - 1),
                )
            nc.scalar.copy(
                out=z_rows[ib][:, c * K_PASS : (c + 1) * K_PASS].rearrange("i (u p e) -> i u p e", u=2, e=2),
                in_=zt[:].rearrange("i (p u e) -> i u p e", u=2, e=2),
            )
            return ib, c, zt

        def square(ib, c, zt):
            squares = work.tile([P, BS], F32, name="squares", tag="squares")
            nc.scalar.activation(out=squares[:], in_=zt[:], func=ACT.Square, accum_out=n_parts[:, ib, c : c + 1])

        def norm_columns(blocks):
            some = slice(blocks[0], blocks[-1] + 1)
            nc.vector.tensor_reduce(out=n_col[:, some], in_=n_parts[:, some, :], op=ALU.add, axis=AX.X)

        def norm_rows(blocks, copy):
            spread = acc_pool.tile([P, BS], F32, name="spread", tag="acc")
            for ib in blocks:
                own = slice(ib * P, (ib + 1) * P)
                nc.tensor.transpose(spread[:, own], n_col[:, ib : ib + 1].to_broadcast([P, P]), ident[:])
            some = slice(blocks[0] * P, (blocks[-1] + 1) * P)
            if blocks[-1] < BLOCKS - 1:
                copy(out=n_rows[:, some], in_=spread[:, some])
            for ib in blocks:
                own = slice(ib * P, (ib + 1) * P)
                nc.vector.tensor_add(out=n_diag[:, own], in0=spread[:, own], in1=off_scale[:])

        dist = keep.tile([P, BLOCKS, BS], F32)
        gram_of = {}

        def gram(ib, chunks, lo=0, hi=None):
            hi = (ib + 1) * P if hi is None else hi
            if (ib, lo) not in gram_of:
                if lo == 0:
                    gram_of[ib, lo] = acc_pool.tile([P, BS], F32, name="gram", tag="acc")
                else:
                    gram_of[ib, lo] = flip_pool.tile([P, BS], F32, name="gram_part", tag="flip")
            rows = slice(ib * P, (ib + 1) * P)
            for c in chunks:
                nc.tensor.matmul_mx(
                    out=gram_of[ib, lo][:, lo:hi],
                    lhsT=z_codes[c][:, rows].bitcast(FP8X4),
                    lhsT_scale=z_scales[c][:, rows],
                    rhs=z_codes[c][:, lo:hi].bitcast(FP8X4),
                    rhs_scale=z_scales[c][:, lo:hi],
                    start=(c == 0),
                    stop=(c == CHUNKS - 1),
                )

        def squared(ib, lo, hi):
            own = ib * P
            bank = gram_of.get((ib, lo), gram_of[ib, 0])
            sq = work.tile([P, BS], F32, name="sq", tag="sq", bufs=4)
            for a, b, row in ((lo, min(hi, own), n_rows), (max(lo, own), hi, n_diag)):
                if a < b:
                    nc.vector.scalar_tensor_tensor(
                        out=sq[:, a:b], in0=bank[:, a:b], scalar=-2.0, in1=row[:, a:b], op0=ALU.mult, op1=ALU.add
                    )
            return ib, lo, hi, sq

        def rooted(ib, lo, hi, sq):
            if ib == 2:
                nc.scalar.activation(out=sq[:, lo:hi], in_=sq[:, lo:hi], func=ACT.Relu, bias=n_col[:, ib : ib + 1])
            else:
                nc.vector.tensor_scalar(
                    out=sq[:, lo:hi], in0=sq[:, lo:hi], scalar1=n_col[:, ib : ib + 1], scalar2=0.0, op0=ALU.add, op1=ALU.max
                )
            nc.scalar.activation(out=dist[:, ib, lo:hi], in_=sq[:, lo:hi], func=ACT.Sqrt, bias=sqrt_floor[:])

        def distances(pieces):
            before = None
            for piece in pieces:
                now = squared(*piece)
                if before is not None:
                    rooted(*before)
                before = now
            rooted(*before)

        def mirror(ib, lo=0, hi=None):
            hi = ib if hi is None else hi
            own = slice(ib * P, (ib + 1) * P)
            mirrored = flip_pool.tile([P, BLOCKS, P], F32, name="mirrored", tag="flip")
            for jb in range(lo, hi):
                nc.tensor.transpose(mirrored[:, jb, :], dist[:, ib, jb * P : (jb + 1) * P], ident[:])
            nc.vector.tensor_copy(out=dist[:, lo:hi, own], in_=mirrored[:, lo:hi, :])

        every = range(CHUNKS)
        warm_up(5)
        f0 = flip_features(0, 1)
        warm_up(2)
        unload(f0, scalar=(1, 3))
        quantise(f0)
        square(*project(0, 0))
        f1 = flip_features(1, 2)
        warm_up(1)
        unload(f1)
        quantise(f1)
        square(*project(0, 1))
        square(*project(1, 0))
        square(*project(1, 1))
        square(*project(0, 2))
        order_features(2)
        square(*project(1, 2))
        x2 = flip_features(2, 2)
        za = flip_z(0, (0, 1)) + flip_z(1, (0, 1))
        unload(x2)
        unload(za[:1])
        quantise(x2)
        unload(za[1:], scalar=(0,))
        quantise(za)
        square(*project(0, 3))
        square(*project(1, 3))
        order_features(3)
        square(*project(2, 0))
        square(*project(2, 1))
        norm_columns([0, 1])
        x3 = flip_features(3, 2)
        zb = flip_z(0, (2, 3)) + flip_z(1, (2, 3))
        unload(x3)
        unload(zb[:1])
        quantise(x3)
        unload(zb[1:], scalar=(0,))
        norm_rows([0, 1], nc.vector.tensor_copy)
        quantise(zb)
        square(*project(2, 2))
        square(*project(2, 3))
        square(*project(3, 0))
        gram(0, every)
        gram(1, every)
        distances([(0, 0, 128), (1, 0, 256)])
        square(*project(3, 1))
        norm_columns([2])
        z2 = flip_z(2, (0, 1)) + flip_z(2, (2, 3)) + flip_z(3, (0,))
        unload(z2)
        quantise(z2)
        norm_rows([2], nc.scalar.copy)
        z32 = project(3, 2)
        z33 = project(3, 3)
        square(*z32)
        square(*z33)
        z31 = flip_z(3, (1,))
        z32 = flip_z(3, (2,))
        unload(z31)
        gram(2, every, 0, 256)
        unload(z32)
        quantise(z31 + z32)
        z33 = flip_z(3, (3,))
        unload(z33)
        gram(3, (0,))
        gram(2, every, 256, 384)
        quantise(z33)
        near = squared(2, 0, 256)
        norm_columns([3])
        rooted(*near)
        gram(3, (1, 2, 3))
        own_2 = squared(2, 256, 384)
        rooted(*own_2)
        others_3 = squared(3, 0, 384)
        norm_rows([3], None)
        rooted(*others_3)
        distances([(3, 384, 512)])
        mirror(1)
        mirror(2)
        mirror(3, 0, 2)
        mirror(3, 2, 3)
        warm_up(6)

        adj = keep.tile([P, BLOCKS, BS], F32)
        normalized = keep.tile([P, BLOCKS, BS], F32)
        scaled = keep.tile([P, BLOCKS, BS // 2], F32)
        deg = keep.tile([P, BLOCKS], F32)
        inv_sqrt_deg = keep.tile([P, BLOCKS], F32)

        def adjacency(ib):
            one = slice(ib, ib + 1)
            nc.scalar.activation(out=adj[:, ib, :], in_=dist[:, ib, :], func=ACT.Exp, scale=-1.0, accum_out=deg[:, one])
            nc.sync.dma_start(out=out_1[ib * P : (ib + 1) * P, :], in_=adj[:, ib, :])
            nc.gpsimd.tensor_tensor(out=inv_sqrt_deg[:, one], in0=deg[:, one], in1=minus_half[:, one], op=ALU.pow)

        def inv_row(bank, k, ib):
            nc.tensor.transpose(bank[:, k * P : (k + 1) * P], inv_sqrt_deg[:, ib : ib + 1].to_broadcast([P, P]), ident[:])

        def scale_rows(ib, width):
            nc.vector.tensor_scalar(
                out=scaled[:, ib, 0:width], in0=adj[:, ib, 0:width], scalar1=inv_sqrt_deg[:, ib : ib + 1], scalar2=0.0,
                op0=ALU.mult, op1=ALU.add,
            )

        def both(ib, lo, hi, inv):
            nc.vector.scalar_tensor_tensor(
                out=normalized[:, ib, lo:hi], in0=adj[:, ib, lo:hi], scalar=inv_sqrt_deg[:, ib : ib + 1], in1=inv,
                op0=ALU.mult, op1=ALU.mult,
            )

        def scale_columns(first, jb, inv):
            n = BLOCKS - first
            cols = slice(jb * P, (jb + 1) * P)
            nc.vector.tensor_tensor(
                out=normalized[:, first:, cols], in0=scaled[:, first:, cols],
                in1=inv.unsqueeze(1).to_broadcast([P, n, P]), op=ALU.mult,
            )

        def by_symmetry(bank, jb, blocks):
            for ib in blocks:
                nc.tensor.transpose(bank[:, ib, :], scaled[:, ib, jb * P : (jb + 1) * P], ident[:])

        def finish_rows(jb, bank):
            nc.scalar.activation(
                out=normalized[:, jb, (jb + 1) * P :], in_=bank[:, jb + 1 :, :].rearrange("p b i -> p (b i)"),
                func=ACT.Copy, scale=inv_sqrt_deg[:, jb : jb + 1],
            )

        def store(first, last, lo, hi):
            nc.sync.dma_start(
                out=out_0[first * P : (last + 1) * P, lo:hi].rearrange("(b p) j -> p b j", p=P),
                in_=normalized[:, first : last + 1, lo:hi],
            )

        adjacency(3)
        adjacency(2)
        adjacency(1)
        adjacency(0)
        turned_1 = acc_pool.tile([P, BLOCKS, P], F32, name="turned_1", tag="acc")
        turned_0 = acc_pool.tile([P, BLOCKS, P], F32, name="turned_0", tag="acc")
        right = flip_pool.tile([P, 2 * P], F32, name="right", tag="flip")
        left_1 = flip_pool.tile([P, P], F32, name="left_1", tag="flip")
        left_0 = flip_pool.tile([P, P], F32, name="left_0", tag="flip")
        inv_row(right, 1, 3)
        scale_rows(3, 2 * P)
        by_symmetry(turned_1, 1, (3,))
        by_symmetry(turned_0, 0, (3,))
        inv_row(right, 0, 2)
        scale_rows(2, 2 * P)
        by_symmetry(turned_1, 1, (2,))
        by_symmetry(turned_0, 0, (2,))
        both(2, 2 * P, BS, right[:])
        store(2, 2, 2 * P, BS)
        inv_row(left_1, 0, 1)
        scale_rows(1, P)
        by_symmetry(turned_0, 0, (1,))
        both(3, 2 * P, BS, right[:])
        store(3, 3, 2 * P, BS)
        finish_rows(1, turned_1)
        store(1, 1, 2 * P, BS)
        scale_columns(2, 1, left_1[:])
        both(1, P, 2 * P, left_1[:])
        store(1, 3, P, 2 * P)
        inv_row(left_0, 0, 0)
        finish_rows(0, turned_0)
        store(0, 0, P, BS)
        scale_columns(1, 0, left_0[:])
        store(1, 3, 0, P)
        both(0, 0, P, left_0[:])
        store(0, 0, 0, P)
